import numpy as np
import ml_dtypes


def mxq(x, axis, fmt="e4m3"):
    dtype, down = {"e4m3": (ml_dtypes.float8_e4m3fn, 7), "e5m2": (ml_dtypes.float8_e5m2, 14)}[fmt]
    v = np.moveaxis(np.asarray(x, np.float32).astype(ml_dtypes.bfloat16).astype(np.float64), axis, -1)
    blocks = v.reshape(v.shape[:-1] + (-1, 32))
    amax = np.abs(blocks).max(-1, keepdims=True)
    byte = np.maximum(np.where(amax > 0, np.frexp(amax)[1] - 1 + 127, 0) - down, 1)
    scale = np.exp2(byte - 127.0)
    codes = (blocks / scale).astype(np.float32).astype(dtype).astype(np.float64)
    return np.moveaxis((codes * scale).reshape(v.shape), -1, axis)


WIDE = False


def mx_kscale(k):
    if not WIDE:
        return np.ones(k)
    levels = np.array([10, -10, 5, -5, 0])
    a = np.random.permutation(np.resize(levels, k // 512 * 4)).reshape(k // 512, 4)
    idx = np.arange(k)
    return np.exp2(a[idx // 512, idx % 128 // 32])


BF16 = ml_dtypes.bfloat16


def bf(x):
    return np.asarray(x, np.float32).astype(BF16)


def f64(x):
    return np.asarray(x).astype(np.float64)


B, C, HD, F, G, O = 128, 4, 4, 1024, 1024, 128
N = C * HD


def setup_inputs():
    s, t = mx_kscale(F), mx_kscale(G)
    return {
        "x": bf(np.random.standard_normal((B, C, HD, F)) * s),
        "W1g": bf(np.random.standard_normal((G, F)) * 0.7 * np.sqrt(N / F) / s * t[:, None]),
        "b1g": bf(np.random.standard_normal(G) * 0.2 * t),
        "W2g": bf(np.random.standard_normal((O, G)) * 1.5 / np.sqrt(G) / t),
        "b2g": bf(np.random.standard_normal(O) * 0.2),
    }


def reference(x, W1g, b1g, W2g, b2g):
    xn = f64(x).reshape(B * N, F)
    y = mxq(xn, 1, "e4m3") @ mxq(f64(W1g), 1, "e4m3").T
    m1 = np.maximum(y.reshape(B, N, G).sum(1) / N + f64(b1g), 0.0)
    m2 = np.maximum((mxq(m1, 1, "e4m3") @ mxq(f64(W2g), 1, "e4m3").T) + f64(b2g), 0.0)
    return np.broadcast_to(m2[:, None, :], (B, N, O)).copy()

@@ -1,0 +1,211 @@
+from contextlib import ExitStack
+
+import concourse.mybir as mybir
+from concourse.masks import make_identity
+
+F32 = mybir.dt.float32
+BF16 = mybir.dt.bfloat16
+U32 = mybir.dt.uint32
+U8 = mybir.dt.uint8
+FP8X4 = mybir.dt.float8_e4m3fn_x4
+ALU = mybir.AluOpType
+ACTF = mybir.ActivationFunctionType
+
+P = 128
+NODES = 16
+FEAT = 1024
+HID = 1024
+OUTF = 128
+FLOPS = 2 * P * NODES * FEAT * HID + 2 * P * HID * OUTF
+
+X_CHUNKS = [(0, 1), (1, 1), (2, 2), (4, 2), (6, 2), (8, 2), (10, 2), (12, 2), (14, 2)]
+W_CHUNKS = [(0, 0, 1), (0, 1, 1), (0, 2, 1), (0, 3, 1), (1, 0, 2), (1, 2, 2)]
+ROUNDS = [[0, 1, 2, 3], [4, 5, 6, 7], [8, 9, 10, 11], [12, 13, 14, 15]]
+REP = 4
+
+
+def tile_gcn_pa_kernel(tc, x, W1g, b1g, W2g, b2g, out):
+    nc = tc.nc
+    with ExitStack() as ctx:
+        keep = ctx.enter_context(tc.tile_pool(name="keep", bufs=1))
+        stage = ctx.enter_context(tc.tile_pool(name="stage", bufs=6))
+        accp = ctx.enter_context(tc.psum_pool(name="accp", bufs=1))
+        tpp = ctx.enter_context(tc.psum_pool(name="tpp", bufs=6))
+        ctx.enter_context(tc.manual_schedule())
+
+        ident_f = keep.tile([P, P], F32, name="ident_f")
+        make_identity(nc, ident_f[:])
+        ident_b = keep.tile([P, P], BF16, name="ident_b")
+        make_identity(nc, ident_b[:])
+        warm_in = keep.tile([P, 8], F32, name="warm_in")
+        warm_out = keep.tile([P, 8], F32, name="warm_out")
+        nc.vector.memset(warm_in[:], 0.0)
+        nc.scalar.copy(out=warm_out[:], in_=warm_in[:])
+
+        w1v = W1g.rearrange("(a p t) k -> a p t k", a=2, p=P, t=4)
+        xv = x.rearrange("b c h f -> b (c h) f")
+        w_raw = {}
+        for a, t0, cnt in W_CHUNKS:
+            wt = keep.tile([P, cnt, FEAT], BF16, name="wraw%d%d" % (a, t0))
+            nc.sync.dma_start(out=wt[:], in_=w1v[a][:, t0 : t0 + cnt, :])
+            for i in range(cnt):
+                w_raw[(a, t0 + i)] = wt[:, i, :]
+        x_raw = {}
+        for n0, cnt in X_CHUNKS:
+            xt = keep.tile([P, cnt, FEAT], BF16, name="xraw%d" % n0)
+            nc.sync.dma_start(out=xt[:], in_=xv[:, n0 : n0 + cnt, :])
+            for i in range(cnt):
+                x_raw[n0 + i] = xt[:, i, :]
+        w2_raw = keep.tile([P, HID], BF16, name="w2_raw")
+        nc.sync.dma_start(out=w2_raw[:], in_=W2g)
+        b1bc = keep.tile([P, HID], BF16, name="b1bc")
+        nc.sync.dma_start(out=b1bc[:], in_=b1g.partition_broadcast(P))
+        b2bc = keep.tile([P, OUTF], BF16, name="b2bc")
+        nc.sync.dma_start(out=b2bc[:], in_=b2g.partition_broadcast(P))
+
+        w1c = [keep.tile([P, 2, 512], U32, name="w1c%d" % a, align_bytes=64) for a in range(2)]
+        w1s = [keep.tile([P, 2, 512], U8, name="w1s%d" % a, align_bytes=64) for a in range(2)]
+        gw = [keep.tile([P, 4096], BF16, name="gw%d" % a, align_bytes=64) for a in range(2)]
+        xc = [keep.tile([P, 2, P], U32, name="xc%d" % n, align_bytes=64) for n in range(NODES)]
+        xs = [keep.tile([P, 2, P], U8, name="xs%d" % n, align_bytes=64) for n in range(NODES)]
+        acc = [accp.tile([P, 512], F32, name="acc%d" % a) for a in range(2)]
+
+        def transpose_words(raw):
+            bank = tpp.tile([P, 4, P], F32, name="bank", tag="tp")
+            words = raw.bitcast(F32)
+            for j in range(4):
+                nc.tensor.transpose(bank[:, j, :], words[:, j * P : (j + 1) * P], ident_f[:])
+            return bank
+
+        def copy_out(eng, dst, bank):
+            src = bank[:].rearrange("p (k u) c -> p k c u", k=2, u=2)
+            if eng == "v":
+                nc.vector.tensor_copy(out=dst, in_=src)
+            else:
+                nc.scalar.copy(out=dst, in_=src)
+
+        def prep_w(a, t):
+            bank = transpose_words(w_raw[(a, t)])
+            dst = gw[a][:].bitcast(F32).rearrange("p (k t c u) -> p k t c u", k=2, t=4, c=P, u=2)
+            copy_out("v" if t == 3 else "s", dst[:, :, t, :, :], bank)
+            if t % 2 == 1:
+                pair = t // 2
+                for kp in range(2):
+                    nc.vector.quantize_mx(
+                        out=w1c[a][:, kp, pair * 256 : (pair + 1) * 256].bitcast(FP8X4),
+                        scales=w1s[a][:, kp, pair * 256 : (pair + 1) * 256],
+                        in_=gw[a][:, kp * 2048 + pair * 1024 : kp * 2048 + (pair + 1) * 1024],
+                    )
+
+        def prep_x(n):
+            bank = transpose_words(x_raw[n])
+            gx = stage.tile([P, 1024], BF16, name="gx", align_bytes=64)
+            dst = gx[:].bitcast(F32).rearrange("p (k c u) -> p k c u", k=2, c=P, u=2)
+            copy_out("s", dst, bank)
+            nc.vector.quantize_mx(
+                out=xc[n][:].rearrange("p k c -> p (k c)").bitcast(FP8X4),
+                scales=xs[n][:].rearrange("p k c -> p (k c)"),
+                in_=gx[:],
+            )
+
+        def mx_pass(n, kp, a):
+            nc.tensor.matmul_mx(
+                out=acc[a][:],
+                lhsT=xc[n][:, kp, :].bitcast(FP8X4),
+                lhsT_scale=xs[n][:, kp, :],
+                rhs=w1c[a][:, kp, :].bitcast(FP8X4),
+                rhs_scale=w1s[a][:, kp, :],
+                start=(n == 0 and kp == 0),
+                stop=(n == NODES - 1 and kp == 1),
+            )
+
+        for a in range(2):
+            for t in range(4):
+                prep_w(a, t)
+        for n in ROUNDS[0]:
+            prep_x(n)
+        for r in range(len(ROUNDS) - 1):
+            for n in ROUNDS[r + 1]:
+                prep_x(n)
+            if r == len(ROUNDS) - 2:
+                w2bank = tpp.tile([P, 4, P], F32, name="w2bank", tag="tp")
+                w2w = w2_raw[:].bitcast(F32).rearrange("p (a w h) -> p a h w", a=2, w=P, h=2)
+                for a in range(2):
+                    for h in range(2):
+                        nc.tensor.transpose(w2bank[:, 2 * a + h, :], w2w[:, a, h, :], ident_f[:])
+                gw2 = keep.tile([P, 1024], BF16, name="gw2", align_bytes=64)
+                copy_out("s", gw2[:].bitcast(F32).rearrange("p (k c u) -> p k c u", k=2, c=P, u=2), w2bank)
+                w2c = keep.tile([P, 2, P], U32, name="w2c", align_bytes=64)
+                w2s = keep.tile([P, 2, P], U8, name="w2s", align_bytes=64)
+                nc.vector.quantize_mx(
+                    out=w2c[:].rearrange("p k c -> p (k c)").bitcast(FP8X4),
+                    scales=w2s[:].rearrange("p k c -> p (k c)"),
+                    in_=gw2[:],
+                )
+            for n in ROUNDS[r]:
+                for kp in range(2):
+                    for a in range(2):
+                        mx_pass(n, kp, a)
+
+        b1v = b1bc[:].rearrange("b (a p t) -> b a t p", a=2, p=P, t=4)
+        hid = [keep.tile([P, 4, P], BF16, name="hid%d" % a) for a in range(2)]
+        g2 = [keep.tile([P, P, 4], BF16, name="g2%d" % a, align_bytes=64) for a in range(2)]
+        m1c = [keep.tile([P, P], U32, name="m1c%d" % a, align_bytes=64) for a in range(2)]
+        m1s = [keep.tile([P, P], U8, name="m1s%d" % a, align_bytes=64) for a in range(2)]
+
+        def bias_mean(a, t0, cnt):
+            nc.vector.scalar_tensor_tensor(
+                out=hid[a][:, t0 : t0 + cnt, :],
+                in0=acc[a][:].rearrange("b (t p) -> b t p", t=4)[:, t0 : t0 + cnt, :],
+                scalar=1.0 / NODES,
+                in1=b1v[:, a, t0 : t0 + cnt, :],
+                op0=ALU.mult,
+                op1=ALU.add,
+            )
+
+        for n in ROUNDS[-1]:
+            for kp in range(2):
+                mx_pass(n, kp, 0)
+        bias_mean(0, 0, 4)
+        for n in ROUNDS[-1]:
+            for kp in range(2):
+                mx_pass(n, kp, 1)
+        bias_mean(1, 0, 2)
+        bias_mean(1, 2, 2)
+
+        hidT = []
+        for a in range(2):
+            ht = tpp.tile([P, 4, P], BF16, name="hidT%d" % a, tag="tp")
+            for t in range(4):
+                nc.tensor.transpose(ht[:, t, :], hid[a][:, t, :], ident_b[:])
+            hidT.append(ht)
+        nc.scalar.activation(out=g2[0][:], in_=hidT[0][:].rearrange("p t b -> p b t"), func=ACTF.Relu)
+        nc.vector.quantize_mx(
+            out=m1c[0][:].bitcast(FP8X4), scales=m1s[0][:], in_=g2[0][:].rearrange("p b t -> p (b t)")
+        )
+        nc.vector.tensor_scalar_max(out=g2[1][:], in0=hidT[1][:].rearrange("p t b -> p b t"), scalar1=0.0)
+        nc.vector.quantize_mx(
+            out=m1c[1][:].bitcast(FP8X4), scales=m1s[1][:], in_=g2[1][:].rearrange("p b t -> p (b t)")
+        )
+
+        acc2 = tpp.tile([P, OUTF], F32, name="acc2", tag="tp")
+        for a in range(2):
+            nc.tensor.matmul_mx(
+                out=acc2[:],
+                lhsT=m1c[a][:].bitcast(FP8X4),
+                lhsT_scale=m1s[a][:],
+                rhs=w2c[:, a, :].bitcast(FP8X4),
+                rhs_scale=w2s[:, a, :],
+                start=(a == 0),
+                stop=(a == 1),
+            )
+        pre = keep.tile([P, OUTF], F32, name="pre")
+        nc.vector.tensor_tensor(out=pre[:], in0=acc2[:], in1=b2bc[:], op=ALU.add)
+        m2r = keep.tile([P, REP, OUTF], F32, name="m2r")
+        nc.vector.tensor_scalar_max(
+            out=m2r[:], in0=pre[:].unsqueeze(1).to_broadcast([P, REP, OUTF]), scalar1=0.0
+        )
+        nc.sync.dma_start(
+            out=out.rearrange("b (i r) o -> b i (r o)", r=REP),
+            in_=m2r[:].rearrange("p r o -> p (r o)").unsqueeze(1).to_broadcast([P, NODES // REP, REP * OUTF]),
+        )

@@ -10,6 +10,7 @@ U8 = mybir.dt.uint8
 FP8X4 = mybir.dt.float8_e4m3fn_x4
 ALU = mybir.AluOpType
 ACTF = mybir.ActivationFunctionType
+AXIS_X = mybir.AxisListType.X
 
 P = 128
 NODES = 16
@@ -19,8 +20,8 @@ OUTF = 128
 FLOPS = 2 * P * NODES * FEAT * HID + 2 * P * HID * OUTF
 
 X_CHUNKS = [(0, 1), (1, 1), (2, 2), (4, 2), (6, 2), (8, 2), (10, 2), (12, 2), (14, 2)]
-W_CHUNKS = [(0, 0, 1), (0, 1, 1), (0, 2, 1), (0, 3, 1), (1, 0, 2), (1, 2, 2)]
-ROUNDS = [[0, 1, 2, 3], [4, 5, 6, 7], [8, 9, 10, 11], [12, 13, 14, 15]]
+W_CHUNKS = {0: [(0, 1), (1, 1), (2, 1), (3, 1)], 1: [(0, 2), (2, 2)]}
+ROUNDS = [[0, 1], [2, 3], [4, 5, 6, 7], [8, 9, 10, 11], [12, 13, 14, 15]]
 REP = 4
 
 
@@ -30,7 +31,7 @@ def tile_gcn_pa_kernel(tc, x, W1g, b1g, W2g, b2g, out):
         keep = ctx.enter_context(tc.tile_pool(name="keep", bufs=1))
         stage = ctx.enter_context(tc.tile_pool(name="stage", bufs=6))
         accp = ctx.enter_context(tc.psum_pool(name="accp", bufs=1))
-        tpp = ctx.enter_context(tc.psum_pool(name="tpp", bufs=6))
+        tpp = ctx.enter_context(tc.psum_pool(name="tpp", bufs=7))
         ctx.enter_context(tc.manual_schedule())
 
         ident_f = keep.tile([P, P], F32, name="ident_f")
@@ -45,30 +46,41 @@ def tile_gcn_pa_kernel(tc, x, W1g, b1g, W2g, b2g, out):
         w1v = W1g.rearrange("(a p t) k -> a p t k", a=2, p=P, t=4)
         xv = x.rearrange("b c h f -> b (c h) f")
         w_raw = {}
-        for a, t0, cnt in W_CHUNKS:
-            wt = keep.tile([P, cnt, FEAT], BF16, name="wraw%d%d" % (a, t0))
-            nc.sync.dma_start(out=wt[:], in_=w1v[a][:, t0 : t0 + cnt, :])
-            for i in range(cnt):
-                w_raw[(a, t0 + i)] = wt[:, i, :]
         x_raw = {}
+
+        def load_w(a):
+            for t0, cnt in W_CHUNKS[a]:
+                wt = keep.tile([P, cnt, FEAT], BF16, name="wraw%d%d" % (a, t0))
+                nc.sync.dma_start(out=wt[:], in_=w1v[a][:, t0 : t0 + cnt, :])
+                for i in range(cnt):
+                    w_raw[(a, t0 + i)] = wt[:, i, :]
+
+        load_w(0)
         for n0, cnt in X_CHUNKS:
             xt = keep.tile([P, cnt, FEAT], BF16, name="xraw%d" % n0)
             nc.sync.dma_start(out=xt[:], in_=xv[:, n0 : n0 + cnt, :])
             for i in range(cnt):
                 x_raw[n0 + i] = xt[:, i, :]
+        load_w(1)
         w2_raw = keep.tile([P, HID], BF16, name="w2_raw")
         nc.sync.dma_start(out=w2_raw[:], in_=W2g)
-        b1bc = keep.tile([P, HID], BF16, name="b1bc")
-        nc.sync.dma_start(out=b1bc[:], in_=b1g.partition_broadcast(P))
+        b1bc = keep.tile([P, 512], BF16, name="b1bc")
+        nc.sync.dma_start(out=b1bc[:], in_=b1g[0:512].partition_broadcast(P))
+        b1c_raw = keep.tile([P, 4], BF16, name="b1c_raw")
+        nc.sync.dma_start(out=b1c_raw[:], in_=b1g[512:1024].rearrange("(p t) -> p t", t=4))
         b2bc = keep.tile([P, OUTF], BF16, name="b2bc")
         nc.sync.dma_start(out=b2bc[:], in_=b2g.partition_broadcast(P))
 
         w1c = [keep.tile([P, 2, 512], U32, name="w1c%d" % a, align_bytes=64) for a in range(2)]
         w1s = [keep.tile([P, 2, 512], U8, name="w1s%d" % a, align_bytes=64) for a in range(2)]
         gw = [keep.tile([P, 4096], BF16, name="gw%d" % a, align_bytes=64) for a in range(2)]
-        xc = [keep.tile([P, 2, P], U32, name="xc%d" % n, align_bytes=64) for n in range(NODES)]
-        xs = [keep.tile([P, 2, P], U8, name="xs%d" % n, align_bytes=64) for n in range(NODES)]
-        acc = [accp.tile([P, 512], F32, name="acc%d" % a) for a in range(2)]
+        xc = {}
+        xs = {}
+        for grp in range(4):
+            for kp in range(2):
+                xc[(grp, kp)] = keep.tile([P, 4, P], U32, name="xc%d%d" % (grp, kp), align_bytes=64)
+                xs[(grp, kp)] = keep.tile([P, 4, P], U8, name="xs%d%d" % (grp, kp), align_bytes=64)
+        acc0 = accp.tile([P, 512], F32, name="acc0")
 
         def transpose_words(raw):
             bank = tpp.tile([P, 4, P], F32, name="bank", tag="tp")
@@ -87,7 +99,7 @@ def tile_gcn_pa_kernel(tc, x, W1g, b1g, W2g, b2g, out):
         def prep_w(a, t):
             bank = transpose_words(w_raw[(a, t)])
             dst = gw[a][:].bitcast(F32).rearrange("p (k t c u) -> p k t c u", k=2, t=4, c=P, u=2)
-            copy_out("v" if t == 3 else "s", dst[:, :, t, :, :], bank)
+            copy_out("v" if t % 2 == 0 else "s", dst[:, :, t, :, :], bank)
             if t % 2 == 1:
                 pair = t // 2
                 for kp in range(2):
@@ -100,34 +112,37 @@ def tile_gcn_pa_kernel(tc, x, W1g, b1g, W2g, b2g, out):
         def prep_x(n):
             bank = transpose_words(x_raw[n])
             gx = stage.tile([P, 1024], BF16, name="gx", align_bytes=64)
-            dst = gx[:].bitcast(F32).rearrange("p (k c u) -> p k c u", k=2, c=P, u=2)
-            copy_out("s", dst, bank)
-            nc.vector.quantize_mx(
-                out=xc[n][:].rearrange("p k c -> p (k c)").bitcast(FP8X4),
-                scales=xs[n][:].rearrange("p k c -> p (k c)"),
-                in_=gx[:],
-            )
+            copy_out("s", gx[:].bitcast(F32).rearrange("p (k c u) -> p k c u", k=2, c=P, u=2), bank)
+            for kp in range(2):
+                nc.vector.quantize_mx(
+                    out=xc[(n // 4, kp)][:, n % 4, :].bitcast(FP8X4),
+                    scales=xs[(n // 4, kp)][:, n % 4, :],
+                    in_=gx[:, kp * 512 : (kp + 1) * 512],
+                )
 
-        def mx_pass(n, kp, a):
-            nc.tensor.matmul_mx(
-                out=acc[a][:],
-                lhsT=xc[n][:, kp, :].bitcast(FP8X4),
-                lhsT_scale=xs[n][:, kp, :],
-                rhs=w1c[a][:, kp, :].bitcast(FP8X4),
-                rhs_scale=w1s[a][:, kp, :],
-                start=(n == 0 and kp == 0),
-                stop=(n == NODES - 1 and kp == 1),
-            )
+        def first_half(n):
+            for kp in range(2):
+                nc.tensor.matmul_mx(
+                    out=acc0[:],
+                    lhsT=xc[(n // 4, kp)][:, n % 4, :].bitcast(FP8X4),
+                    lhsT_scale=xs[(n // 4, kp)][:, n % 4, :],
+                    rhs=w1c[0][:, kp, :].bitcast(FP8X4),
+                    rhs_scale=w1s[0][:, kp, :],
+                    start=(n == 0 and kp == 0),
+                    stop=(n == NODES - 1 and kp == 1),
+                )
 
-        for a in range(2):
-            for t in range(4):
-                prep_w(a, t)
+        for t in range(4):
+            prep_w(0, t)
         for n in ROUNDS[0]:
             prep_x(n)
-        for r in range(len(ROUNDS) - 1):
-            for n in ROUNDS[r + 1]:
-                prep_x(n)
-            if r == len(ROUNDS) - 2:
+        for r in range(len(ROUNDS)):
+            if r + 1 < len(ROUNDS):
+                for n in ROUNDS[r + 1]:
+                    prep_x(n)
+            else:
+                for t in range(4):
+                    prep_w(1, t)
                 w2bank = tpp.tile([P, 4, P], F32, name="w2bank", tag="tp")
                 w2w = w2_raw[:].bitcast(F32).rearrange("p (a w h) -> p a h w", a=2, w=P, h=2)
                 for a in range(2):
@@ -143,55 +158,68 @@ def tile_gcn_pa_kernel(tc, x, W1g, b1g, W2g, b2g, out):
                     in_=gw2[:],
                 )
             for n in ROUNDS[r]:
-                for kp in range(2):
-                    for a in range(2):
-                        mx_pass(n, kp, a)
+                first_half(n)
 
-        b1v = b1bc[:].rearrange("b (a p t) -> b a t p", a=2, p=P, t=4)
-        hid = [keep.tile([P, 4, P], BF16, name="hid%d" % a) for a in range(2)]
         g2 = [keep.tile([P, P, 4], BF16, name="g2%d" % a, align_bytes=64) for a in range(2)]
         m1c = [keep.tile([P, P], U32, name="m1c%d" % a, align_bytes=64) for a in range(2)]
         m1s = [keep.tile([P, P], U8, name="m1s%d" % a, align_bytes=64) for a in range(2)]
+        b1c = keep.tile([P, 4], F32, name="b1c")
+        nc.vector.tensor_copy(out=b1c[:], in_=b1c_raw[:])
+        hid0 = keep.tile([P, 4, P], BF16, name="hid0")
+        nc.vector.scalar_tensor_tensor(
+            out=hid0[:],
+            in0=acc0[:].rearrange("b (t p) -> b t p", t=4),
+            scalar=1.0 / NODES,
+            in1=b1bc[:].rearrange("b (p t) -> b t p", p=P, t=4),
+            op0=ALU.mult,
+            op1=ALU.add,
+        )
 
-        def bias_mean(a, t0, cnt):
-            nc.vector.scalar_tensor_tensor(
-                out=hid[a][:, t0 : t0 + cnt, :],
-                in0=acc[a][:].rearrange("b (t p) -> b t p", t=4)[:, t0 : t0 + cnt, :],
-                scalar=1.0 / NODES,
-                in1=b1v[:, a, t0 : t0 + cnt, :],
-                op0=ALU.mult,
-                op1=ALU.add,
+        def second_half(t, wide):
+            if wide:
+                gb = tpp.tile([P, 4, P], F32, name="gb", tag="tp")
+                for grp in range(4):
+                    for kp in range(2):
+                        nc.tensor.matmul_mx(
+                            out=gb[:].rearrange("p s b -> p (s b)"),
+                            lhsT=w1c[1][:, kp, t * P : (t + 1) * P].bitcast(FP8X4),
+                            lhsT_scale=w1s[1][:, kp, t * P : (t + 1) * P],
+                            rhs=xc[(grp, kp)][:].rearrange("p s b -> p (s b)").bitcast(FP8X4),
+                            rhs_scale=xs[(grp, kp)][:].rearrange("p s b -> p (s b)"),
+                            start=(grp == 0 and kp == 0),
+                            stop=(grp == 3 and kp == 1),
+                        )
+                total = stage.tile([P, P], F32, name="total")
+                nc.vector.tensor_reduce(out=total[:], in_=gb[:].rearrange("p s b -> p b s"), axis=AXIS_X, op=ALU.add)
+            else:
+                total = tpp.tile([P, P], F32, name="gn", tag="tp")
+                for n in range(NODES):
+                    for kp in range(2):
+                        nc.tensor.matmul_mx(
+                            out=total[:],
+                            lhsT=w1c[1][:, kp, t * P : (t + 1) * P].bitcast(FP8X4),
+                            lhsT_scale=w1s[1][:, kp, t * P : (t + 1) * P],
+                            rhs=xc[(n // 4, kp)][:, n % 4, :].bitcast(FP8X4),
+                            rhs_scale=xs[(n // 4, kp)][:, n % 4, :],
+                            start=(n == 0 and kp == 0),
+                            stop=(n == NODES - 1 and kp == 1),
+                        )
+            nc.scalar.activation(
+                out=g2[1][:, :, t], in_=total[:], func=ACTF.Relu, bias=b1c[:, t : t + 1], scale=1.0 / NODES
             )
 
-        for n in ROUNDS[-1]:
-            for kp in range(2):
-                mx_pass(n, kp, 0)
-        bias_mean(0, 0, 4)
-        for n in ROUNDS[-1]:
-            for kp in range(2):
-                mx_pass(n, kp, 1)
-        bias_mean(1, 0, 2)
-        bias_mean(1, 2, 2)
+        def quantise_hidden(a):
+            nc.vector.quantize_mx(
+                out=m1c[a][:].bitcast(FP8X4), scales=m1s[a][:], in_=g2[a][:].rearrange("p b t -> p (b t)")
+            )
 
-        hidT = []
-        for a in range(2):
-            ht = tpp.tile([P, 4, P], BF16, name="hidT%d" % a, tag="tp")
-            for t in range(4):
-                nc.tensor.transpose(ht[:, t, :], hid[a][:, t, :], ident_b[:])
-            hidT.append(ht)
-        nc.scalar.activation(out=g2[0][:], in_=hidT[0][:].rearrange("p t b -> p b t"), func=ACTF.Relu)
-        nc.vector.quantize_mx(
-            out=m1c[0][:].bitcast(FP8X4), scales=m1s[0][:], in_=g2[0][:].rearrange("p b t -> p (b t)")
-        )
-        nc.vector.tensor_scalar_max(out=g2[1][:], in0=hidT[1][:].rearrange("p t b -> p b t"), scalar1=0.0)
-        nc.vector.quantize_mx(
-            out=m1c[1][:].bitcast(FP8X4), scales=m1s[1][:], in_=g2[1][:].rearrange("p b t -> p (b t)")
-        )
+        acc2_box = []
 
-        acc2 = tpp.tile([P, OUTF], F32, name="acc2", tag="tp")
-        for a in range(2):
+        def layer2(a):
+            if a == 0:
+                acc2_box.append(tpp.tile([P, OUTF], F32, name="acc2", tag="tp"))
             nc.tensor.matmul_mx(
-                out=acc2[:],
+                out=acc2_box[0][:],
                 lhsT=m1c[a][:].bitcast(FP8X4),
                 lhsT_scale=m1s[a][:],
                 rhs=w2c[:, a, :].bitcast(FP8X4),
@@ -199,8 +227,22 @@ def tile_gcn_pa_kernel(tc, x, W1g, b1g, W2g, b2g, out):
                 start=(a == 0),
                 stop=(a == 1),
             )
+
+        second_half(0, True)
+        second_half(1, True)
+        hidT = tpp.tile([P, 4, P], BF16, name="hidT", tag="tp")
+        for t in range(4):
+            nc.tensor.transpose(hidT[:, t, :], hid0[:, t, :], ident_b[:])
+        nc.scalar.activation(out=g2[0][:], in_=hidT[:].rearrange("p t b -> p b t"), func=ACTF.Relu)
+        quantise_hidden(0)
+        second_half(2, True)
+        layer2(0)
+        second_half(3, False)
+        quantise_hidden(1)
+        layer2(1)
+
         pre = keep.tile([P, OUTF], F32, name="pre")
-        nc.vector.tensor_tensor(out=pre[:], in0=acc2[:], in1=b2bc[:], op=ALU.add)
+        nc.vector.tensor_tensor(out=pre[:], in0=acc2_box[0][:], in1=b2bc[:], op=ALU.add)
         m2r = keep.tile([P, REP, OUTF], F32, name="m2r")
         nc.vector.tensor_scalar_max(
             out=m2r[:], in0=pre[:].unsqueeze(1).to_broadcast([P, REP, OUTF]), scalar1=0.0

@@ -23,6 +23,7 @@ X_CHUNKS = [(0, 1), (1, 1), (2, 2), (4, 2), (6, 2), (8, 2), (10, 2), (12, 2), (1
 W_CHUNKS = {0: [(0, 1), (1, 1), (2, 1), (3, 1)], 1: [(0, 2), (2, 2)]}
 ROUNDS = [[0, 1], [2, 3], [4, 5, 6, 7], [8, 9, 10, 11], [12, 13, 14, 15]]
 REP = 4
+WARM_FIRST = 5
 
 
 def tile_gcn_pa_kernel(tc, x, W1g, b1g, W2g, b2g, out):
@@ -41,6 +42,8 @@ def tile_gcn_pa_kernel(tc, x, W1g, b1g, W2g, b2g, out):
         warm_in = keep.tile([P, 8], F32, name="warm_in")
         warm_out = keep.tile([P, 8], F32, name="warm_out")
         nc.vector.memset(warm_in[:], 0.0)
+        zeros = keep.tile([P, 512], BF16, name="zeros")
+        nc.vector.memset(zeros[:], 0.0)
         nc.scalar.copy(out=warm_out[:], in_=warm_in[:])
 
         w1v = W1g.rearrange("(a p t) k -> a p t k", a=2, p=P, t=4)
@@ -132,13 +135,23 @@ def tile_gcn_pa_kernel(tc, x, W1g, b1g, W2g, b2g, out):
                     stop=(n == NODES - 1 and kp == 1),
                 )
 
+        def keep_busy(count):
+            for i in range(count):
+                nc.tensor.matmul(acc0[:], lhsT=zeros[:, 0:P], rhs=zeros[:], start=True, stop=True)
+
+        keep_busy(WARM_FIRST)
         for t in range(4):
+            if t > 0:
+                keep_busy(1)
             prep_w(0, t)
         for n in ROUNDS[0]:
+            keep_busy(1)
             prep_x(n)
         for r in range(len(ROUNDS)):
             if r + 1 < len(ROUNDS):
                 for n in ROUNDS[r + 1]:
+                    if r == 0:
+                        keep_busy(1)
                     prep_x(n)
             else:
                 for t in range(4):

@@ -21,7 +21,7 @@ FLOPS = 2 * P * NODES * FEAT * HID + 2 * P * HID * OUTF
 
 X_CHUNKS = [(0, 1), (1, 1), (2, 2), (4, 2), (6, 2), (8, 2), (10, 2), (12, 2), (14, 2)]
 W_CHUNKS = {0: [(0, 1), (1, 1), (2, 1), (3, 1)], 1: [(0, 2), (2, 2)]}
-ROUNDS = [[0, 1], [2, 3], [4, 5, 6, 7], [8, 9, 10, 11], [12, 13, 14, 15]]
+RUNS = [[0, 1], [2, 3, 4, 5, 6, 7], [8, 9, 10, 11, 12, 13, 14, 15]]
 REP = 4
 WARM_FIRST = 5
 
@@ -30,7 +30,7 @@ def tile_gcn_pa_kernel(tc, x, W1g, b1g, W2g, b2g, out):
     nc = tc.nc
     with ExitStack() as ctx:
         keep = ctx.enter_context(tc.tile_pool(name="keep", bufs=1))
-        stage = ctx.enter_context(tc.tile_pool(name="stage", bufs=6))
+        stage = ctx.enter_context(tc.tile_pool(name="stage", bufs=8))
         accp = ctx.enter_context(tc.psum_pool(name="accp", bufs=1))
         tpp = ctx.enter_context(tc.psum_pool(name="tpp", bufs=7))
         ctx.enter_context(tc.manual_schedule())
@@ -46,7 +46,7 @@ def tile_gcn_pa_kernel(tc, x, W1g, b1g, W2g, b2g, out):
         nc.vector.memset(zeros[:], 0.0)
         nc.scalar.copy(out=warm_out[:], in_=warm_in[:])
 
-        w1v = W1g.rearrange("(a p t) k -> a p t k", a=2, p=P, t=4)
+        w1v = W1g.rearrange("(a u p e) k -> a p u e k", a=2, u=2, p=P, e=2)
         xv = x.rearrange("b c h f -> b (c h) f")
         w_raw = {}
         x_raw = {}
@@ -54,7 +54,7 @@ def tile_gcn_pa_kernel(tc, x, W1g, b1g, W2g, b2g, out):
         def load_w(a):
             for t0, cnt in W_CHUNKS[a]:
                 wt = keep.tile([P, cnt, FEAT], BF16, name="wraw%d%d" % (a, t0))
-                nc.sync.dma_start(out=wt[:], in_=w1v[a][:, t0 : t0 + cnt, :])
+                nc.sync.dma_start(out=wt[:], in_=w1v[a][:, t0 // 2, t0 % 2 : t0 % 2 + cnt, :])
                 for i in range(cnt):
                     w_raw[(a, t0 + i)] = wt[:, i, :]
 
@@ -69,8 +69,8 @@ def tile_gcn_pa_kernel(tc, x, W1g, b1g, W2g, b2g, out):
         nc.sync.dma_start(out=w2_raw[:], in_=W2g)
         b1bc = keep.tile([P, 512], BF16, name="b1bc")
         nc.sync.dma_start(out=b1bc[:], in_=b1g[0:512].partition_broadcast(P))
-        b1c_raw = keep.tile([P, 4], BF16, name="b1c_raw")
-        nc.sync.dma_start(out=b1c_raw[:], in_=b1g[512:1024].rearrange("(p t) -> p t", t=4))
+        b1c_raw = keep.tile([P, 2, 2], BF16, name="b1c_raw")
+        nc.sync.dma_start(out=b1c_raw[:], in_=b1g[512:1024].rearrange("(u p e) -> p u e", u=2, p=P, e=2))
         b2bc = keep.tile([P, OUTF], BF16, name="b2bc")
         nc.sync.dma_start(out=b2bc[:], in_=b2g.partition_broadcast(P))
 
@@ -144,49 +144,54 @@ def tile_gcn_pa_kernel(tc, x, W1g, b1g, W2g, b2g, out):
             if t > 0:
                 keep_busy(1)
             prep_w(0, t)
-        for n in ROUNDS[0]:
-            keep_busy(1)
-            prep_x(n)
-        for r in range(len(ROUNDS)):
-            if r + 1 < len(ROUNDS):
-                for n in ROUNDS[r + 1]:
-                    if r == 0:
-                        keep_busy(1)
-                    prep_x(n)
-            else:
-                for t in range(4):
-                    prep_w(1, t)
-                w2bank = tpp.tile([P, 4, P], F32, name="w2bank", tag="tp")
-                w2w = w2_raw[:].bitcast(F32).rearrange("p (a w h) -> p a h w", a=2, w=P, h=2)
-                for a in range(2):
-                    for h in range(2):
-                        nc.tensor.transpose(w2bank[:, 2 * a + h, :], w2w[:, a, h, :], ident_f[:])
-                gw2 = keep.tile([P, 1024], BF16, name="gw2", align_bytes=64)
-                copy_out("s", gw2[:].bitcast(F32).rearrange("p (k c u) -> p k c u", k=2, c=P, u=2), w2bank)
-                w2c = keep.tile([P, 2, P], U32, name="w2c", align_bytes=64)
-                w2s = keep.tile([P, 2, P], U8, name="w2s", align_bytes=64)
-                nc.vector.quantize_mx(
-                    out=w2c[:].rearrange("p k c -> p (k c)").bitcast(FP8X4),
-                    scales=w2s[:].rearrange("p k c -> p (k c)"),
-                    in_=gw2[:],
-                )
-            for n in ROUNDS[r]:
+        for run in RUNS:
+            for n in run:
+                if n < 2:
+                    keep_busy(1)
+                prep_x(n)
+            for n in run:
                 first_half(n)
 
         g2 = [keep.tile([P, P, 4], BF16, name="g2%d" % a, align_bytes=64) for a in range(2)]
         m1c = [keep.tile([P, P], U32, name="m1c%d" % a, align_bytes=64) for a in range(2)]
         m1s = [keep.tile([P, P], U8, name="m1s%d" % a, align_bytes=64) for a in range(2)]
-        b1c = keep.tile([P, 4], F32, name="b1c")
-        nc.vector.tensor_copy(out=b1c[:], in_=b1c_raw[:])
         hid0 = keep.tile([P, 4, P], BF16, name="hid0")
-        nc.vector.scalar_tensor_tensor(
-            out=hid0[:],
-            in0=acc0[:].rearrange("b (t p) -> b t p", t=4),
-            scalar=1.0 / NODES,
-            in1=b1bc[:].rearrange("b (p t) -> b t p", p=P, t=4),
-            op0=ALU.mult,
-            op1=ALU.add,
+        b1v = b1bc[:].rearrange("b (u p e) -> b u e p", u=2, p=P, e=2)
+        for u in range(2):
+            nc.vector.scalar_tensor_tensor(
+                out=hid0[:, 2 * u : 2 * u + 2, :],
+                in0=acc0[:].rearrange("b (t p) -> b t p", t=4)[:, 2 * u : 2 * u + 2, :],
+                scalar=1.0 / NODES,
+                in1=b1v[:, u, :, :],
+                op0=ALU.mult,
+                op1=ALU.add,
+            )
+
+        for t in range(4):
+            prep_w(1, t)
+        w2bank = transpose_words(w2_raw[:])
+        gw2 = keep.tile([P, 1024], BF16, name="gw2", align_bytes=64)
+        copy_out("s", gw2[:].bitcast(F32).rearrange("p (k c u) -> p k c u", k=2, c=P, u=2), w2bank)
+        w2c = keep.tile([P, 2, P], U32, name="w2c", align_bytes=64)
+        w2s = keep.tile([P, 2, P], U8, name="w2s", align_bytes=64)
+        nc.vector.quantize_mx(
+            out=w2c[:].rearrange("p k c -> p (k c)").bitcast(FP8X4),
+            scales=w2s[:].rearrange("p k c -> p (k c)"),
+            in_=gw2[:],
         )
+        hidT = tpp.tile([P, 4, P], BF16, name="hidT", tag="tp")
+        for t in range(4):
+            nc.tensor.transpose(hidT[:, t, :], hid0[:, t, :], ident_b[:])
+        nc.scalar.activation(out=g2[0][:], in_=hidT[:].rearrange("p t b -> p b t"), func=ACTF.Relu)
+
+        def quantise_hidden(a):
+            nc.vector.quantize_mx(
+                out=m1c[a][:].bitcast(FP8X4), scales=m1s[a][:], in_=g2[a][:].rearrange("p b t -> p (b t)")
+            )
+
+        quantise_hidden(0)
+        b1c = keep.tile([P, 4], F32, name="b1c")
+        nc.vector.tensor_copy(out=b1c[:], in_=b1c_raw[:].rearrange("p u e -> p (u e)"))
 
         def second_half(t, wide):
             if wide:
@@ -221,18 +226,9 @@ def tile_gcn_pa_kernel(tc, x, W1g, b1g, W2g, b2g, out):
                 out=g2[1][:, :, t], in_=total[:], func=ACTF.Relu, bias=b1c[:, t : t + 1], scale=1.0 / NODES
             )
 
-        def quantise_hidden(a):
-            nc.vector.quantize_mx(
-                out=m1c[a][:].bitcast(FP8X4), scales=m1s[a][:], in_=g2[a][:].rearrange("p b t -> p (b t)")
-            )
-
-        acc2_box = []
-
         def layer2(a):
-            if a == 0:
-                acc2_box.append(tpp.tile([P, OUTF], F32, name="acc2", tag="tp"))
             nc.tensor.matmul_mx(
-                out=acc2_box[0][:],
+                out=acc2[:],
                 lhsT=m1c[a][:].bitcast(FP8X4),
                 lhsT_scale=m1s[a][:],
                 rhs=w2c[:, a, :].bitcast(FP8X4),
@@ -243,19 +239,15 @@ def tile_gcn_pa_kernel(tc, x, W1g, b1g, W2g, b2g, out):
 
         second_half(0, True)
         second_half(1, True)
-        hidT = tpp.tile([P, 4, P], BF16, name="hidT", tag="tp")
-        for t in range(4):
-            nc.tensor.transpose(hidT[:, t, :], hid0[:, t, :], ident_b[:])
-        nc.scalar.activation(out=g2[0][:], in_=hidT[:].rearrange("p t b -> p b t"), func=ACTF.Relu)
-        quantise_hidden(0)
-        second_half(2, True)
+        acc2 = tpp.tile([P, OUTF], F32, name="acc2", tag="tp")
         layer2(0)
+        second_half(2, True)
         second_half(3, False)
         quantise_hidden(1)
         layer2(1)
 
         pre = keep.tile([P, OUTF], F32, name="pre")
-        nc.vector.tensor_tensor(out=pre[:], in0=acc2_box[0][:], in1=b2bc[:], op=ALU.add)
+        nc.vector.tensor_tensor(out=pre[:], in0=acc2[:], in1=b2bc[:], op=ALU.add)
         m2r = keep.tile([P, REP, OUTF], F32, name="m2r")
         nc.vector.tensor_scalar_max(
             out=m2r[:], in0=pre[:].unsqueeze(1).to_broadcast([P, REP, OUTF]), scalar1=0.0

@@ -19,11 +19,11 @@ HID = 1024
 OUTF = 128
 FLOPS = 2 * P * NODES * FEAT * HID + 2 * P * HID * OUTF
 
-X_CHUNKS = [(0, 1), (1, 1), (2, 2), (4, 2), (6, 2), (8, 2), (10, 2), (12, 2), (14, 2)]
-W_CHUNKS = {0: [(0, 1), (1, 1), (2, 1), (3, 1)], 1: [(0, 2), (2, 2)]}
-RUNS = [[0, 1], [2, 3, 4, 5, 6, 7], [8, 9, 10, 11, 12, 13, 14, 15]]
+X_CHUNKS = [(0, 2), (2, 2), (4, 2), (6, 2), (8, 2), (10, 2), (12, 2), (14, 2)]
+W_CHUNKS = {0: [(0, 2), (2, 2)], 1: [(0, 2), (2, 2)]}
+ROUNDS = [[0, 1], [2, 3], [4, 5, 6, 7], [8, 9, 10, 11], [12, 13, 14, 15]]
 REP = 4
-WARM_FIRST = 5
+WARM_FIRST = 7
 
 
 def tile_gcn_pa_kernel(tc, x, W1g, b1g, W2g, b2g, out):
@@ -141,20 +141,27 @@ def tile_gcn_pa_kernel(tc, x, W1g, b1g, W2g, b2g, out):
 
         keep_busy(WARM_FIRST)
         for t in range(4):
-            if t > 0:
-                keep_busy(1)
             prep_w(0, t)
-        for run in RUNS:
-            for n in run:
-                if n < 2:
-                    keep_busy(1)
-                prep_x(n)
-            for n in run:
+            if t % 2 == 1:
+                keep_busy(2)
+        for n in ROUNDS[0]:
+            prep_x(n)
+        keep_busy(1)
+        for r in range(len(ROUNDS)):
+            if r + 1 < len(ROUNDS):
+                for n in ROUNDS[r + 1]:
+                    prep_x(n)
+            else:
+                for t in range(4):
+                    prep_w(1, t)
+            for n in ROUNDS[r]:
                 first_half(n)
 
         g2 = [keep.tile([P, P, 4], BF16, name="g2%d" % a, align_bytes=64) for a in range(2)]
         m1c = [keep.tile([P, P], U32, name="m1c%d" % a, align_bytes=64) for a in range(2)]
         m1s = [keep.tile([P, P], U8, name="m1s%d" % a, align_bytes=64) for a in range(2)]
+        b1c = keep.tile([P, 4], F32, name="b1c")
+        nc.vector.tensor_copy(out=b1c[:], in_=b1c_raw[:].rearrange("p u e -> p (u e)"))
         hid0 = keep.tile([P, 4, P], BF16, name="hid0")
         b1v = b1bc[:].rearrange("b (u p e) -> b u e p", u=2, p=P, e=2)
         for u in range(2):
@@ -167,31 +174,10 @@ def tile_gcn_pa_kernel(tc, x, W1g, b1g, W2g, b2g, out):
                 op1=ALU.add,
             )
 
-        for t in range(4):
-            prep_w(1, t)
-        w2bank = transpose_words(w2_raw[:])
-        gw2 = keep.tile([P, 1024], BF16, name="gw2", align_bytes=64)
-        copy_out("s", gw2[:].bitcast(F32).rearrange("p (k c u) -> p k c u", k=2, c=P, u=2), w2bank)
-        w2c = keep.tile([P, 2, P], U32, name="w2c", align_bytes=64)
-        w2s = keep.tile([P, 2, P], U8, name="w2s", align_bytes=64)
-        nc.vector.quantize_mx(
-            out=w2c[:].rearrange("p k c -> p (k c)").bitcast(FP8X4),
-            scales=w2s[:].rearrange("p k c -> p (k c)"),
-            in_=gw2[:],
-        )
-        hidT = tpp.tile([P, 4, P], BF16, name="hidT", tag="tp")
-        for t in range(4):
-            nc.tensor.transpose(hidT[:, t, :], hid0[:, t, :], ident_b[:])
-        nc.scalar.activation(out=g2[0][:], in_=hidT[:].rearrange("p t b -> p b t"), func=ACTF.Relu)
-
         def quantise_hidden(a):
             nc.vector.quantize_mx(
                 out=m1c[a][:].bitcast(FP8X4), scales=m1s[a][:], in_=g2[a][:].rearrange("p b t -> p (b t)")
             )
-
-        quantise_hidden(0)
-        b1c = keep.tile([P, 4], F32, name="b1c")
-        nc.vector.tensor_copy(out=b1c[:], in_=b1c_raw[:].rearrange("p u e -> p (u e)"))
 
         def second_half(t, wide):
             if wide:
@@ -226,6 +212,28 @@ def tile_gcn_pa_kernel(tc, x, W1g, b1g, W2g, b2g, out):
                 out=g2[1][:, :, t], in_=total[:], func=ACTF.Relu, bias=b1c[:, t : t + 1], scale=1.0 / NODES
             )
 
+        second_half(0, True)
+
+        hidT = tpp.tile([P, 4, P], BF16, name="hidT", tag="tp")
+        for t in range(4):
+            nc.tensor.transpose(hidT[:, t, :], hid0[:, t, :], ident_b[:])
+        nc.scalar.activation(out=g2[0][:], in_=hidT[:].rearrange("p t b -> p b t"), func=ACTF.Relu)
+        quantise_hidden(0)
+        w2bank = transpose_words(w2_raw[:])
+        gw2 = keep.tile([P, 1024], BF16, name="gw2", align_bytes=64)
+        copy_out("s", gw2[:].bitcast(F32).rearrange("p (k c u) -> p k c u", k=2, c=P, u=2), w2bank)
+        w2c = keep.tile([P, 2, P], U32, name="w2c", align_bytes=64)
+        w2s = keep.tile([P, 2, P], U8, name="w2s", align_bytes=64)
+        nc.vector.quantize_mx(
+            out=w2c[:].rearrange("p k c -> p (k c)").bitcast(FP8X4),
+            scales=w2s[:].rearrange("p k c -> p (k c)"),
+            in_=gw2[:],
+        )
+
+        second_half(1, True)
+        second_half(2, True)
+        acc2 = tpp.tile([P, OUTF], F32, name="acc2", tag="tp")
+
         def layer2(a):
             nc.tensor.matmul_mx(
                 out=acc2[:],
@@ -237,11 +245,7 @@ def tile_gcn_pa_kernel(tc, x, W1g, b1g, W2g, b2g, out):
                 stop=(a == 1),
             )
 
-        second_half(0, True)
-        second_half(1, True)
-        acc2 = tpp.tile([P, OUTF], F32, name="acc2", tag="tp")
         layer2(0)
-        second_half(2, True)
         second_half(3, False)
         quantise_hidden(1)
         layer2(1)

@@ -10,229 +10,294 @@ U8 = mybir.dt.uint8
 FP8X4 = mybir.dt.float8_e4m3fn_x4
 ALU = mybir.AluOpType
 ACTF = mybir.ActivationFunctionType
-AXIS_X = mybir.AxisListType.X
 
 P = 128
 NODES = 16
+PAIRS = 8
 FEAT = 1024
 HID = 1024
 OUTF = 128
 FLOPS = 2 * P * NODES * FEAT * HID + 2 * P * HID * OUTF
 
-X_CHUNKS = [(0, 2), (2, 2), (4, 2), (6, 2), (8, 2), (10, 2), (12, 2), (14, 2)]
-W_CHUNKS = {0: [(0, 2), (2, 2)], 1: [(0, 2), (2, 2)]}
-ROUNDS = [[0, 1], [2, 3], [4, 5, 6, 7], [8, 9, 10, 11], [12, 13, 14, 15]]
+NATURAL = 1
 REP = 4
-WARM_FIRST = 7
 
 
 def tile_gcn_pa_kernel(tc, x, W1g, b1g, W2g, b2g, out):
     nc = tc.nc
     with ExitStack() as ctx:
         keep = ctx.enter_context(tc.tile_pool(name="keep", bufs=1))
-        stage = ctx.enter_context(tc.tile_pool(name="stage", bufs=8))
+        stage = ctx.enter_context(tc.tile_pool(name="stage", bufs=4))
         accp = ctx.enter_context(tc.psum_pool(name="accp", bufs=1))
-        tpp = ctx.enter_context(tc.psum_pool(name="tpp", bufs=7))
+        tpp = ctx.enter_context(tc.psum_pool(name="tpp", bufs=5))
         ctx.enter_context(tc.manual_schedule())
+
+        brow = keep.tile([P, HID + OUTF], BF16, name="brow")
+        nc.vector.memset(brow[:], 0.0)
+        nc.scalar.dma_start(out=brow[0:1, 0:HID], in_=b1g.unsqueeze(0))
+        nc.scalar.dma_start(out=brow[0:1, HID : HID + OUTF], in_=b2g.unsqueeze(0))
+
+        w1v = W1g.rearrange("(a u p e) k -> a p u e k", a=2, u=2, p=P, e=2)
+        xq = x.rearrange("(i j) c h (q k) -> q i (j c h) k", i=32, j=4, q=4)
+        xn = x.rearrange("b c h f -> b (c h) f")
+        w_raw = {}
+        x_raw = {}
+
+        def load_w(a, u):
+            wt = keep.tile([P, 2, FEAT], BF16, name="wraw%d%d" % (a, u))
+            nc.sync.dma_start(out=wt[:], in_=w1v[a][:, u, :, :])
+            for e in range(2):
+                w_raw[(a, 2 * u + e)] = wt[:, e, :]
+
+        def load_x(m):
+            if m < NATURAL:
+                xt = keep.tile([P, 2, FEAT], BF16, name="xraw%d" % m)
+                nc.sync.dma_start(out=xt[:], in_=xn[:, m:NODES:8, :])
+            else:
+                xt = keep.tile([P, 8, 256], BF16, name="xraw%d" % m, align_bytes=64)
+                for q in (0, 2, 1, 3):
+                    nc.sync.dma_start(out=xt[32 * q : 32 * q + 32, :, :], in_=xq[q][:, m : 4 * NODES : 8, :])
+            x_raw[m] = xt
+
+        load_w(0, 0)
+        load_w(0, 1)
+        load_x(0)
+        load_w(1, 0)
+        load_w(1, 1)
+        for m in range(1, 6):
+            load_x(m)
+        w2_raw = keep.tile([P, HID], BF16, name="w2_raw")
+        nc.sync.dma_start(out=w2_raw[:], in_=W2g)
+        for m in range(6, PAIRS):
+            load_x(m)
 
         ident_f = keep.tile([P, P], F32, name="ident_f")
         make_identity(nc, ident_f[:])
         ident_b = keep.tile([P, P], BF16, name="ident_b")
         make_identity(nc, ident_b[:])
+        ones = keep.tile([P, P], BF16, name="ones")
+        nc.vector.memset(ones[:], 1.0)
         warm_in = keep.tile([P, 8], F32, name="warm_in")
         warm_out = keep.tile([P, 8], F32, name="warm_out")
         nc.vector.memset(warm_in[:], 0.0)
         zeros = keep.tile([P, 512], BF16, name="zeros")
         nc.vector.memset(zeros[:], 0.0)
         nc.scalar.copy(out=warm_out[:], in_=warm_in[:])
-
-        w1v = W1g.rearrange("(a u p e) k -> a p u e k", a=2, u=2, p=P, e=2)
-        xv = x.rearrange("b c h f -> b (c h) f")
-        w_raw = {}
-        x_raw = {}
-
-        def load_w(a):
-            for t0, cnt in W_CHUNKS[a]:
-                wt = keep.tile([P, cnt, FEAT], BF16, name="wraw%d%d" % (a, t0))
-                nc.sync.dma_start(out=wt[:], in_=w1v[a][:, t0 // 2, t0 % 2 : t0 % 2 + cnt, :])
-                for i in range(cnt):
-                    w_raw[(a, t0 + i)] = wt[:, i, :]
-
-        load_w(0)
-        for n0, cnt in X_CHUNKS:
-            xt = keep.tile([P, cnt, FEAT], BF16, name="xraw%d" % n0)
-            nc.sync.dma_start(out=xt[:], in_=xv[:, n0 : n0 + cnt, :])
-            for i in range(cnt):
-                x_raw[n0 + i] = xt[:, i, :]
-        load_w(1)
-        w2_raw = keep.tile([P, HID], BF16, name="w2_raw")
-        nc.sync.dma_start(out=w2_raw[:], in_=W2g)
-        b1bc = keep.tile([P, 512], BF16, name="b1bc")
-        nc.sync.dma_start(out=b1bc[:], in_=b1g[0:512].partition_broadcast(P))
-        b1c_raw = keep.tile([P, 2, 2], BF16, name="b1c_raw")
-        nc.sync.dma_start(out=b1c_raw[:], in_=b1g[512:1024].rearrange("(u p e) -> p u e", u=2, p=P, e=2))
-        b2bc = keep.tile([P, OUTF], BF16, name="b2bc")
-        nc.sync.dma_start(out=b2bc[:], in_=b2g.partition_broadcast(P))
+        perm_f = keep.tile([P, P], F32, name="perm_f")
+        nc.scalar.copy(out=perm_f[:].rearrange("p (j i) -> p j i", j=4), in_=ident_f[:].rearrange("p (i j) -> p j i", j=4))
+        perm_b = keep.tile([P, P], BF16, name="perm_b")
+        nc.scalar.copy(out=perm_b[:].rearrange("p (i j) -> p i j", j=4), in_=ident_b[:].rearrange("p (j i) -> p i j", j=4))
 
         w1c = [keep.tile([P, 2, 512], U32, name="w1c%d" % a, align_bytes=64) for a in range(2)]
         w1s = [keep.tile([P, 2, 512], U8, name="w1s%d" % a, align_bytes=64) for a in range(2)]
         gw = [keep.tile([P, 4096], BF16, name="gw%d" % a, align_bytes=64) for a in range(2)]
         xc = {}
         xs = {}
-        for grp in range(4):
-            for kp in range(2):
-                xc[(grp, kp)] = keep.tile([P, 4, P], U32, name="xc%d%d" % (grp, kp), align_bytes=64)
-                xs[(grp, kp)] = keep.tile([P, 4, P], U8, name="xs%d%d" % (grp, kp), align_bytes=64)
-        acc0 = accp.tile([P, 512], F32, name="acc0")
+        for m in range(PAIRS):
+            xc[m] = keep.tile([P, 2, 2, P], U32, name="xc%d" % m, align_bytes=64)
+            xs[m] = keep.tile([P, 2, 2, P], U8, name="xs%d" % m, align_bytes=64)
+        acc = [accp.tile([P, 512], F32, name="acc%d" % a) for a in range(2)]
 
-        def transpose_words(raw):
+        def keep_busy(count):
+            for i in range(count):
+                nc.tensor.matmul(acc[0][:], lhsT=zeros[:, 0:P], rhs=zeros[:], start=True, stop=True)
+
+        def transpose_words(words, identity):
             bank = tpp.tile([P, 4, P], F32, name="bank", tag="tp")
-            words = raw.bitcast(F32)
             for j in range(4):
-                nc.tensor.transpose(bank[:, j, :], words[:, j * P : (j + 1) * P], ident_f[:])
+                nc.tensor.transpose(bank[:, j, :], words[:, j * P : (j + 1) * P], identity[:])
             return bank
 
         def copy_out(eng, dst, bank):
-            src = bank[:].rearrange("p (k u) c -> p k c u", k=2, u=2)
+            src = bank[:].rearrange("p (u k) c -> p k c u", u=2, k=2)
             if eng == "v":
                 nc.vector.tensor_copy(out=dst, in_=src)
             else:
                 nc.scalar.copy(out=dst, in_=src)
 
-        def prep_w(a, t):
-            bank = transpose_words(w_raw[(a, t)])
-            dst = gw[a][:].bitcast(F32).rearrange("p (k t c u) -> p k t c u", k=2, t=4, c=P, u=2)
-            copy_out("v" if t % 2 == 0 else "s", dst[:, :, t, :, :], bank)
-            if t % 2 == 1:
-                pair = t // 2
-                for kp in range(2):
-                    nc.vector.quantize_mx(
-                        out=w1c[a][:, kp, pair * 256 : (pair + 1) * 256].bitcast(FP8X4),
-                        scales=w1s[a][:, kp, pair * 256 : (pair + 1) * 256],
-                        in_=gw[a][:, kp * 2048 + pair * 1024 : kp * 2048 + (pair + 1) * 1024],
-                    )
+        def permute_words(eng, raw):
+            wp = stage.tile([P, 4, 4, 64], BF16, name="wp")
+            src = raw.rearrange("p (q b k) -> p b q k", q=4, b=4)
+            if eng == "v":
+                nc.vector.tensor_copy(out=wp[:], in_=src)
+            else:
+                nc.scalar.copy(out=wp[:], in_=src)
+            return wp[:].rearrange("p b q k -> p (b q k)").bitcast(F32)
 
-        def prep_x(n):
-            bank = transpose_words(x_raw[n])
-            gx = stage.tile([P, 1024], BF16, name="gx", align_bytes=64)
-            copy_out("s", gx[:].bitcast(F32).rearrange("p (k c u) -> p k c u", k=2, c=P, u=2), bank)
+        w_words = {}
+
+        def permute_w(a, t, eng="v"):
+            w_words[(a, t)] = permute_words(eng, w_raw[(a, t)])
+
+        def turn_w(a, t, eng):
+            bank = transpose_words(w_words[(a, t)], ident_f)
+            dst = gw[a][:].bitcast(F32).rearrange("p (k t c u) -> p k t c u", k=2, t=4, c=P, u=2)
+            copy_out(eng, dst[:, :, t, :, :], bank)
+
+        def quant_w(a, pair):
             for kp in range(2):
                 nc.vector.quantize_mx(
-                    out=xc[(n // 4, kp)][:, n % 4, :].bitcast(FP8X4),
-                    scales=xs[(n // 4, kp)][:, n % 4, :],
-                    in_=gx[:, kp * 512 : (kp + 1) * 512],
+                    out=w1c[a][:, kp, pair * 256 : (pair + 1) * 256].bitcast(FP8X4),
+                    scales=w1s[a][:, kp, pair * 256 : (pair + 1) * 256],
+                    in_=gw[a][:, kp * 2048 + pair * 1024 : kp * 2048 + (pair + 1) * 1024],
                 )
 
-        def first_half(n):
-            for kp in range(2):
-                nc.tensor.matmul_mx(
-                    out=acc0[:],
-                    lhsT=xc[(n // 4, kp)][:, n % 4, :].bitcast(FP8X4),
-                    lhsT_scale=xs[(n // 4, kp)][:, n % 4, :],
-                    rhs=w1c[0][:, kp, :].bitcast(FP8X4),
-                    rhs_scale=w1s[0][:, kp, :],
-                    start=(n == 0 and kp == 0),
-                    stop=(n == NODES - 1 and kp == 1),
-                )
+        x_words = {}
+        x_g = {}
 
-        def keep_busy(count):
-            for i in range(count):
-                nc.tensor.matmul(acc0[:], lhsT=zeros[:, 0:P], rhs=zeros[:], start=True, stop=True)
-
-        keep_busy(WARM_FIRST)
-        for t in range(4):
-            prep_w(0, t)
-            if t % 2 == 1:
-                keep_busy(2)
-        for n in ROUNDS[0]:
-            prep_x(n)
-        keep_busy(1)
-        for r in range(len(ROUNDS)):
-            if r + 1 < len(ROUNDS):
-                for n in ROUNDS[r + 1]:
-                    prep_x(n)
+        def stage_a(m, eng="v"):
+            if m < NATURAL:
+                x_words[m] = [permute_words(eng, x_raw[m][:, h, :]) for h in range(2)]
             else:
-                for t in range(4):
-                    prep_w(1, t)
-            for n in ROUNDS[r]:
-                first_half(n)
+                xt = stage.tile([P, 1024], F32, name="xt", align_bytes=64)
+                nc.vector.transpose(out=xt[:], in_=x_raw[m][:].rearrange("p r k -> p (r k)").bitcast(F32))
+                x_words[m] = xt
+
+        def stage_b(m):
+            gx = stage.tile([P, 2, 2, 512], BF16, name="gx", align_bytes=64)
+            x_g[m] = gx
+            for h in range(2):
+                if m < NATURAL:
+                    bank = transpose_words(x_words[m][h], perm_f)
+                    copy_out(
+                        "s",
+                        gx[:, h, :, :].rearrange("p k w -> p (k w)").bitcast(F32).rearrange("p (k c u) -> p k c u", k=2, u=2),
+                        bank,
+                    )
+                else:
+                    src = x_words[m][:].rearrange("p (j h u k i) -> p h k j i u", j=4, h=2, u=2, k=2, i=32)
+                    for kp in range(2):
+                        dst = gx[:, h, kp, :].bitcast(F32).rearrange("p (j i u) -> p j i u", j=4, i=32, u=2)
+                        nc.scalar.copy(out=dst, in_=src[:, h, kp, :, :, :])
+
+        def stage_c(m, h=None):
+            sel = slice(0, 2) if h is None else slice(h, h + 1)
+            nc.vector.quantize_mx(
+                out=xc[m][:, sel, :, :].rearrange("p h k c -> p (h k c)").bitcast(FP8X4),
+                scales=xs[m][:, sel, :, :].rearrange("p h k c -> p (h k c)"),
+                in_=x_g[m][:, sel, :, :].rearrange("p h k c -> p (h k c)"),
+            )
+
+        def passes(m, a, hs=(0, 1)):
+            for h in hs:
+                for kp in range(2):
+                    nc.tensor.matmul_mx(
+                        out=acc[a][:],
+                        lhsT=xc[m][:, h, kp, :].bitcast(FP8X4),
+                        lhsT_scale=xs[m][:, h, kp, :],
+                        rhs=w1c[a][:, kp, :].bitcast(FP8X4),
+                        rhs_scale=w1s[a][:, kp, :],
+                        start=(m == 0 and h == 0 and kp == 0),
+                        stop=(m == PAIRS - 1 and h == 1 and kp == 1),
+                    )
+
+        b1sb = keep.tile([P, 2, 512], F32, name="b1sb")
+        b2sb = keep.tile([P, OUTF], F32, name="b2sb")
+        keep_busy(4)
+        for a in range(2):
+            bb = tpp.tile([P, 512], F32, name="bb", tag="tp")
+            nc.tensor.matmul(bb[:], lhsT=ones[:], rhs=brow[:, a * 512 : (a + 1) * 512], start=True, stop=True)
+            nc.scalar.copy(
+                out=b1sb[:, a, :].rearrange("b (u e p) -> b u e p", u=2, e=2),
+                in_=bb[:].rearrange("b (u p e) -> b u e p", u=2, p=P, e=2),
+            )
+        bb2 = tpp.tile([P, OUTF], F32, name="bb2", tag="tp")
+        nc.tensor.matmul(bb2[:], lhsT=ones[:], rhs=brow[:, HID : HID + OUTF], start=True, stop=True)
+        nc.scalar.copy(out=b2sb[:], in_=bb2[:])
+
+        w2_state = {}
+
+        def turn_w2():
+            w2bank = transpose_words(w2_raw[:].bitcast(F32), ident_f)
+            gw2 = keep.tile([P, 1024], BF16, name="gw2", align_bytes=64)
+            nc.scalar.copy(
+                out=gw2[:].bitcast(F32).rearrange("p (k c u) -> p k c u", k=2, c=P, u=2),
+                in_=w2bank[:].rearrange("p (k u) c -> p k c u", k=2, u=2),
+            )
+            w2_state["g"] = gw2
+
+        def quant_w2():
+            nc.vector.quantize_mx(
+                out=w2c[:].rearrange("p k c -> p (k c)").bitcast(FP8X4),
+                scales=w2s[:].rearrange("p k c -> p (k c)"),
+                in_=w2_state["g"][:],
+            )
+
+        w2c = keep.tile([P, 2, P], U32, name="w2c", align_bytes=64)
+        w2s = keep.tile([P, 2, P], U8, name="w2s", align_bytes=64)
+
+        permute_w(0, 0)
+        permute_w(0, 1)
+        turn_w(0, 0, "s")
+        turn_w(0, 1, "s")
+        permute_w(0, 2)
+        permute_w(0, 3)
+        turn_w(0, 2, "s")
+        turn_w(0, 3, "s")
+        stage_a(0)
+        quant_w(0, 0)
+        stage_b(0)
+        permute_w(1, 0, "v")
+        permute_w(1, 1, "v")
+        quant_w(0, 1)
+        stage_c(0)
+        turn_w(1, 0, "s")
+        turn_w(1, 1, "s")
+        permute_w(1, 2, "v")
+        permute_w(1, 3, "v")
+        stage_a(1)
+        passes(0, 0)
+        turn_w(1, 2, "s")
+        turn_w(1, 3, "s")
+        quant_w(1, 0)
+        stage_b(1)
+        quant_w(1, 1)
+        stage_a(2)
+        stage_c(1)
+        passes(0, 1)
+        for m in range(1, PAIRS):
+            if m + 1 < PAIRS:
+                stage_b(m + 1)
+            if m + 2 < PAIRS:
+                stage_a(m + 2)
+            passes(m, 0)
+            if m < PAIRS - 2:
+                passes(m, 1)
+            if m == 6:
+                turn_w2()
+            if m + 1 < PAIRS - 1:
+                stage_c(m + 1)
+            elif m + 1 < PAIRS:
+                stage_c(m + 1, 0)
+                stage_c(m + 1, 1)
+                quant_w2()
 
         g2 = [keep.tile([P, P, 4], BF16, name="g2%d" % a, align_bytes=64) for a in range(2)]
         m1c = [keep.tile([P, P], U32, name="m1c%d" % a, align_bytes=64) for a in range(2)]
         m1s = [keep.tile([P, P], U8, name="m1s%d" % a, align_bytes=64) for a in range(2)]
-        b1c = keep.tile([P, 4], F32, name="b1c")
-        nc.vector.tensor_copy(out=b1c[:], in_=b1c_raw[:].rearrange("p u e -> p (u e)"))
-        hid0 = keep.tile([P, 4, P], BF16, name="hid0")
-        b1v = b1bc[:].rearrange("b (u p e) -> b u e p", u=2, p=P, e=2)
-        for u in range(2):
+
+        def mean_bias(a):
+            hid = keep.tile([P, 4, P], BF16, name="hid%d" % a)
             nc.vector.scalar_tensor_tensor(
-                out=hid0[:, 2 * u : 2 * u + 2, :],
-                in0=acc0[:].rearrange("b (t p) -> b t p", t=4)[:, 2 * u : 2 * u + 2, :],
+                out=hid[:].rearrange("b t p -> b (t p)"),
+                in0=acc[a][:],
                 scalar=1.0 / NODES,
-                in1=b1v[:, u, :, :],
+                in1=b1sb[:, a, :],
                 op0=ALU.mult,
                 op1=ALU.add,
             )
+            return hid
 
-        def quantise_hidden(a):
+        def turn_hidden(a, hid):
+            hid_t = tpp.tile([P, 4, P], BF16, name="hidT", tag="tp")
+            for t in range(4):
+                nc.tensor.transpose(hid_t[:, t, :], hid[:, t, :], perm_b[:])
+            nc.scalar.activation(out=g2[a][:], in_=hid_t[:].rearrange("p t b -> p b t"), func=ACTF.Relu)
             nc.vector.quantize_mx(
                 out=m1c[a][:].bitcast(FP8X4), scales=m1s[a][:], in_=g2[a][:].rearrange("p b t -> p (b t)")
             )
 
-        def second_half(t, wide):
-            if wide:
-                gb = tpp.tile([P, 4, P], F32, name="gb", tag="tp")
-                for grp in range(4):
-                    for kp in range(2):
-                        nc.tensor.matmul_mx(
-                            out=gb[:].rearrange("p s b -> p (s b)"),
-                            lhsT=w1c[1][:, kp, t * P : (t + 1) * P].bitcast(FP8X4),
-                            lhsT_scale=w1s[1][:, kp, t * P : (t + 1) * P],
-                            rhs=xc[(grp, kp)][:].rearrange("p s b -> p (s b)").bitcast(FP8X4),
-                            rhs_scale=xs[(grp, kp)][:].rearrange("p s b -> p (s b)"),
-                            start=(grp == 0 and kp == 0),
-                            stop=(grp == 3 and kp == 1),
-                        )
-                total = stage.tile([P, P], F32, name="total")
-                nc.vector.tensor_reduce(out=total[:], in_=gb[:].rearrange("p s b -> p b s"), axis=AXIS_X, op=ALU.add)
-            else:
-                total = tpp.tile([P, P], F32, name="gn", tag="tp")
-                for n in range(NODES):
-                    for kp in range(2):
-                        nc.tensor.matmul_mx(
-                            out=total[:],
-                            lhsT=w1c[1][:, kp, t * P : (t + 1) * P].bitcast(FP8X4),
-                            lhsT_scale=w1s[1][:, kp, t * P : (t + 1) * P],
-                            rhs=xc[(n // 4, kp)][:, n % 4, :].bitcast(FP8X4),
-                            rhs_scale=xs[(n // 4, kp)][:, n % 4, :],
-                            start=(n == 0 and kp == 0),
-                            stop=(n == NODES - 1 and kp == 1),
-                        )
-            nc.scalar.activation(
-                out=g2[1][:, :, t], in_=total[:], func=ACTF.Relu, bias=b1c[:, t : t + 1], scale=1.0 / NODES
-            )
-
-        second_half(0, True)
-
-        hidT = tpp.tile([P, 4, P], BF16, name="hidT", tag="tp")
-        for t in range(4):
-            nc.tensor.transpose(hidT[:, t, :], hid0[:, t, :], ident_b[:])
-        nc.scalar.activation(out=g2[0][:], in_=hidT[:].rearrange("p t b -> p b t"), func=ACTF.Relu)
-        quantise_hidden(0)
-        w2bank = transpose_words(w2_raw[:])
-        gw2 = keep.tile([P, 1024], BF16, name="gw2", align_bytes=64)
-        copy_out("s", gw2[:].bitcast(F32).rearrange("p (k c u) -> p k c u", k=2, c=P, u=2), w2bank)
-        w2c = keep.tile([P, 2, P], U32, name="w2c", align_bytes=64)
-        w2s = keep.tile([P, 2, P], U8, name="w2s", align_bytes=64)
-        nc.vector.quantize_mx(
-            out=w2c[:].rearrange("p k c -> p (k c)").bitcast(FP8X4),
-            scales=w2s[:].rearrange("p k c -> p (k c)"),
-            in_=gw2[:],
-        )
-
-        second_half(1, True)
-        second_half(2, True)
-        acc2 = tpp.tile([P, OUTF], F32, name="acc2", tag="tp")
+        acc2 = accp.tile([P, OUTF], F32, name="acc2")
 
         def layer2(a):
             nc.tensor.matmul_mx(
@@ -245,13 +310,17 @@ def tile_gcn_pa_kernel(tc, x, W1g, b1g, W2g, b2g, out):
                 stop=(a == 1),
             )
 
+        hid0 = mean_bias(0)
+        passes(PAIRS - 2, 1)
+        turn_hidden(0, hid0)
+        passes(PAIRS - 1, 1)
+        hid1 = mean_bias(1)
         layer2(0)
-        second_half(3, False)
-        quantise_hidden(1)
+        turn_hidden(1, hid1)
         layer2(1)
 
         pre = keep.tile([P, OUTF], F32, name="pre")
-        nc.vector.tensor_tensor(out=pre[:], in0=acc2[:], in1=b2bc[:], op=ALU.add)
+        nc.vector.tensor_tensor(out=pre[:], in0=acc2[:], in1=b2sb[:], op=ALU.add)
         m2r = keep.tile([P, REP, OUTF], F32, name="m2r")
         nc.vector.tensor_scalar_max(
             out=m2r[:], in0=pre[:].unsqueeze(1).to_broadcast([P, REP, OUTF]), scalar1=0.0

@@ -10,6 +10,7 @@ U8 = mybir.dt.uint8
 FP8X4 = mybir.dt.float8_e4m3fn_x4
 ALU = mybir.AluOpType
 ACTF = mybir.ActivationFunctionType
+AXIS_X = mybir.AxisListType.X
 
 P = 128
 NODES = 16
@@ -19,8 +20,9 @@ HID = 1024
 OUTF = 128
 FLOPS = 2 * P * NODES * FEAT * HID + 2 * P * HID * OUTF
 
-NATURAL = 1
+NATURAL = 2
 REP = 4
+WARM = 8
 
 
 def tile_gcn_pa_kernel(tc, x, W1g, b1g, W2g, b2g, out):
@@ -29,13 +31,8 @@ def tile_gcn_pa_kernel(tc, x, W1g, b1g, W2g, b2g, out):
         keep = ctx.enter_context(tc.tile_pool(name="keep", bufs=1))
         stage = ctx.enter_context(tc.tile_pool(name="stage", bufs=4))
         accp = ctx.enter_context(tc.psum_pool(name="accp", bufs=1))
-        tpp = ctx.enter_context(tc.psum_pool(name="tpp", bufs=5))
+        tpp = ctx.enter_context(tc.psum_pool(name="tpp", bufs=6))
         ctx.enter_context(tc.manual_schedule())
-
-        brow = keep.tile([P, HID + OUTF], BF16, name="brow")
-        nc.vector.memset(brow[:], 0.0)
-        nc.scalar.dma_start(out=brow[0:1, 0:HID], in_=b1g.unsqueeze(0))
-        nc.scalar.dma_start(out=brow[0:1, HID : HID + OUTF], in_=b2g.unsqueeze(0))
 
         w1v = W1g.rearrange("(a u p e) k -> a p u e k", a=2, u=2, p=P, e=2)
         xq = x.rearrange("(i j) c h (q k) -> q i (j c h) k", i=32, j=4, q=4)
@@ -43,11 +40,12 @@ def tile_gcn_pa_kernel(tc, x, W1g, b1g, W2g, b2g, out):
         w_raw = {}
         x_raw = {}
 
-        def load_w(a, u):
-            wt = keep.tile([P, 2, FEAT], BF16, name="wraw%d%d" % (a, u))
-            nc.sync.dma_start(out=wt[:], in_=w1v[a][:, u, :, :])
-            for e in range(2):
-                w_raw[(a, 2 * u + e)] = wt[:, e, :]
+        def load_w(a, t):
+            cnt = 1 if a == 0 else 2
+            wt = keep.tile([P, cnt, FEAT], BF16, name="wraw%d%d" % (a, t))
+            nc.sync.dma_start(out=wt[:], in_=w1v[a][:, t // 2, t % 2 : t % 2 + cnt, :])
+            for e in range(cnt):
+                w_raw[(a, t + e)] = wt[:, e, :]
 
         def load_x(m):
             if m < NATURAL:
@@ -59,29 +57,33 @@ def tile_gcn_pa_kernel(tc, x, W1g, b1g, W2g, b2g, out):
                     nc.sync.dma_start(out=xt[32 * q : 32 * q + 32, :, :], in_=xq[q][:, m : 4 * NODES : 8, :])
             x_raw[m] = xt
 
-        load_w(0, 0)
-        load_w(0, 1)
-        load_x(0)
+        for t in range(4):
+            load_w(0, t)
+        for m in range(2):
+            load_x(m)
         load_w(1, 0)
-        load_w(1, 1)
-        for m in range(1, 6):
+        load_w(1, 2)
+        for m in range(2, PAIRS):
             load_x(m)
         w2_raw = keep.tile([P, HID], BF16, name="w2_raw")
         nc.sync.dma_start(out=w2_raw[:], in_=W2g)
-        for m in range(6, PAIRS):
-            load_x(m)
+        b1bc = keep.tile([P, 512], BF16, name="b1bc")
+        nc.sync.dma_start(out=b1bc[:], in_=b1g[0:512].partition_broadcast(P))
+        b1c_raw = keep.tile([P, 2, 2], BF16, name="b1c_raw")
+        nc.sync.dma_start(out=b1c_raw[:], in_=b1g[512:1024].rearrange("(u p e) -> p u e", u=2, p=P, e=2))
+        b2bc = keep.tile([P, OUTF], BF16, name="b2bc")
+        nc.sync.dma_start(out=b2bc[:], in_=b2g.partition_broadcast(P))
+        b1c = keep.tile([P, 4], F32, name="b1c")
 
+        zeros = keep.tile([P, 512], BF16, name="zeros")
+        nc.vector.memset(zeros[:].bitcast(F32), 0.0)
         ident_f = keep.tile([P, P], F32, name="ident_f")
         make_identity(nc, ident_f[:])
         ident_b = keep.tile([P, P], BF16, name="ident_b")
         make_identity(nc, ident_b[:])
-        ones = keep.tile([P, P], BF16, name="ones")
-        nc.vector.memset(ones[:], 1.0)
         warm_in = keep.tile([P, 8], F32, name="warm_in")
         warm_out = keep.tile([P, 8], F32, name="warm_out")
         nc.vector.memset(warm_in[:], 0.0)
-        zeros = keep.tile([P, 512], BF16, name="zeros")
-        nc.vector.memset(zeros[:], 0.0)
         nc.scalar.copy(out=warm_out[:], in_=warm_in[:])
         perm_f = keep.tile([P, P], F32, name="perm_f")
         nc.scalar.copy(out=perm_f[:].rearrange("p (j i) -> p j i", j=4), in_=ident_f[:].rearrange("p (i j) -> p j i", j=4))
@@ -96,11 +98,11 @@ def tile_gcn_pa_kernel(tc, x, W1g, b1g, W2g, b2g, out):
         for m in range(PAIRS):
             xc[m] = keep.tile([P, 2, 2, P], U32, name="xc%d" % m, align_bytes=64)
             xs[m] = keep.tile([P, 2, 2, P], U8, name="xs%d" % m, align_bytes=64)
-        acc = [accp.tile([P, 512], F32, name="acc%d" % a) for a in range(2)]
+        acc0 = accp.tile([P, 512], F32, name="acc0")
 
         def keep_busy(count):
             for i in range(count):
-                nc.tensor.matmul(acc[0][:], lhsT=zeros[:, 0:P], rhs=zeros[:], start=True, stop=True)
+                nc.tensor.matmul(acc0[:], lhsT=zeros[:, 0:P], rhs=zeros[:], start=True, stop=True)
 
         def transpose_words(words, identity):
             bank = tpp.tile([P, 4, P], F32, name="bank", tag="tp")
@@ -142,6 +144,14 @@ def tile_gcn_pa_kernel(tc, x, W1g, b1g, W2g, b2g, out):
                     in_=gw[a][:, kp * 2048 + pair * 1024 : kp * 2048 + (pair + 1) * 1024],
                 )
 
+        def quant_w_whole(a):
+            for kp in range(2):
+                nc.vector.quantize_mx(
+                    out=w1c[a][:, kp, :].bitcast(FP8X4),
+                    scales=w1s[a][:, kp, :],
+                    in_=gw[a][:, kp * 2048 : (kp + 1) * 2048],
+                )
+
         x_words = {}
         x_g = {}
 
@@ -159,51 +169,123 @@ def tile_gcn_pa_kernel(tc, x, W1g, b1g, W2g, b2g, out):
             for h in range(2):
                 if m < NATURAL:
                     bank = transpose_words(x_words[m][h], perm_f)
-                    copy_out(
-                        "s",
-                        gx[:, h, :, :].rearrange("p k w -> p (k w)").bitcast(F32).rearrange("p (k c u) -> p k c u", k=2, u=2),
-                        bank,
-                    )
+                    dst = gx[:].rearrange("p k h w -> p (k h w)").bitcast(F32).rearrange("p (k h c u) -> p h k c u", k=2, h=2, u=2)
+                    copy_out("s", dst[:, h, :, :, :], bank)
                 else:
                     src = x_words[m][:].rearrange("p (j h u k i) -> p h k j i u", j=4, h=2, u=2, k=2, i=32)
                     for kp in range(2):
-                        dst = gx[:, h, kp, :].bitcast(F32).rearrange("p (j i u) -> p j i u", j=4, i=32, u=2)
+                        dst = gx[:, kp, h, :].bitcast(F32).rearrange("p (j i u) -> p j i u", j=4, i=32, u=2)
                         nc.scalar.copy(out=dst, in_=src[:, h, kp, :, :, :])
 
-        def stage_c(m, h=None):
-            sel = slice(0, 2) if h is None else slice(h, h + 1)
+        def stage_c(m):
             nc.vector.quantize_mx(
-                out=xc[m][:, sel, :, :].rearrange("p h k c -> p (h k c)").bitcast(FP8X4),
-                scales=xs[m][:, sel, :, :].rearrange("p h k c -> p (h k c)"),
-                in_=x_g[m][:, sel, :, :].rearrange("p h k c -> p (h k c)"),
+                out=xc[m][:].rearrange("p k n c -> p (k n c)").bitcast(FP8X4),
+                scales=xs[m][:].rearrange("p k n c -> p (k n c)"),
+                in_=x_g[m][:].rearrange("p k h w -> p (k h w)"),
             )
 
-        def passes(m, a, hs=(0, 1)):
-            for h in hs:
+        def first_half(m):
+            for h in range(2):
                 for kp in range(2):
                     nc.tensor.matmul_mx(
-                        out=acc[a][:],
-                        lhsT=xc[m][:, h, kp, :].bitcast(FP8X4),
-                        lhsT_scale=xs[m][:, h, kp, :],
-                        rhs=w1c[a][:, kp, :].bitcast(FP8X4),
-                        rhs_scale=w1s[a][:, kp, :],
+                        out=acc0[:],
+                        lhsT=xc[m][:, kp, h, :].bitcast(FP8X4),
+                        lhsT_scale=xs[m][:, kp, h, :],
+                        rhs=w1c[0][:, kp, :].bitcast(FP8X4),
+                        rhs_scale=w1s[0][:, kp, :],
                         start=(m == 0 and h == 0 and kp == 0),
                         stop=(m == PAIRS - 1 and h == 1 and kp == 1),
                     )
 
-        b1sb = keep.tile([P, 2, 512], F32, name="b1sb")
-        b2sb = keep.tile([P, OUTF], F32, name="b2sb")
-        keep_busy(4)
-        for a in range(2):
-            bb = tpp.tile([P, 512], F32, name="bb", tag="tp")
-            nc.tensor.matmul(bb[:], lhsT=ones[:], rhs=brow[:, a * 512 : (a + 1) * 512], start=True, stop=True)
-            nc.scalar.copy(
-                out=b1sb[:, a, :].rearrange("b (u e p) -> b u e p", u=2, e=2),
-                in_=bb[:].rearrange("b (u p e) -> b u e p", u=2, p=P, e=2),
+        sums = {}
+
+        def second_half(m, t):
+            if m == 0:
+                sums[t] = tpp.tile([P, 2, P], F32, name="sum", tag="tp")
+            for kp in range(2):
+                nc.tensor.matmul_mx(
+                    out=sums[t][:].rearrange("p s b -> p (s b)"),
+                    lhsT=w1c[1][:, kp, t * P : (t + 1) * P].bitcast(FP8X4),
+                    lhsT_scale=w1s[1][:, kp, t * P : (t + 1) * P],
+                    rhs=xc[m][:, kp, :, :].rearrange("p s b -> p (s b)").bitcast(FP8X4),
+                    rhs_scale=xs[m][:, kp, :, :].rearrange("p s b -> p (s b)"),
+                    start=(m == 0 and kp == 0),
+                    stop=(m == PAIRS - 1 and kp == 1),
+                )
+
+        def second_half_narrow(m, t):
+            if m == 0:
+                sums[t] = tpp.tile([P, P], F32, name="sum", tag="tp")
+            for h in range(2):
+                for kp in range(2):
+                    nc.tensor.matmul_mx(
+                        out=sums[t][:],
+                        lhsT=w1c[1][:, kp, t * P : (t + 1) * P].bitcast(FP8X4),
+                        lhsT_scale=w1s[1][:, kp, t * P : (t + 1) * P],
+                        rhs=xc[m][:, kp, h, :].bitcast(FP8X4),
+                        rhs_scale=xs[m][:, kp, h, :],
+                        start=(m == 0 and h == 0 and kp == 0),
+                        stop=(m == PAIRS - 1 and h == 1 and kp == 1),
+                    )
+
+        keep_busy(WARM)
+
+        g2 = [keep.tile([P, P, 4], BF16, name="g2%d" % a, align_bytes=64) for a in range(2)]
+        m1c = [keep.tile([P, P], U32, name="m1c%d" % a, align_bytes=64) for a in range(2)]
+        m1s = [keep.tile([P, P], U8, name="m1s%d" % a, align_bytes=64) for a in range(2)]
+        hid0 = keep.tile([P, 4, P], BF16, name="hid0")
+        b1v = b1bc[:].rearrange("b (u p e) -> b u e p", u=2, p=P, e=2)
+
+        def mean_bias():
+            for u in range(2):
+                nc.vector.scalar_tensor_tensor(
+                    out=hid0[:, 2 * u : 2 * u + 2, :],
+                    in0=acc0[:].rearrange("b (t p) -> b t p", t=4)[:, 2 * u : 2 * u + 2, :],
+                    scalar=1.0 / NODES,
+                    in1=b1v[:, u, :, :],
+                    op0=ALU.mult,
+                    op1=ALU.add,
+                )
+
+        def turn_hidden():
+            hid_t = tpp.tile([P, 4, P], BF16, name="hidT", tag="tp")
+            for t in range(4):
+                nc.tensor.transpose(hid_t[:, t, :], hid0[:, t, :], perm_b[:])
+            nc.scalar.activation(out=g2[0][:], in_=hid_t[:].rearrange("p t b -> p b t"), func=ACTF.Relu)
+
+        def quant_hidden(a):
+            nc.vector.quantize_mx(
+                out=m1c[a][:].bitcast(FP8X4), scales=m1s[a][:], in_=g2[a][:].rearrange("p b t -> p (b t)")
             )
-        bb2 = tpp.tile([P, OUTF], F32, name="bb2", tag="tp")
-        nc.tensor.matmul(bb2[:], lhsT=ones[:], rhs=brow[:, HID : HID + OUTF], start=True, stop=True)
-        nc.scalar.copy(out=b2sb[:], in_=bb2[:])
+
+        def finish(t, wide):
+            if wide:
+                total = stage.tile([P, P], F32, name="total")
+                nc.vector.tensor_reduce(
+                    out=total[:], in_=sums[t][:].rearrange("p s b -> p b s"), axis=AXIS_X, op=ALU.add
+                )
+            else:
+                total = sums[t]
+            nc.scalar.activation(
+                out=g2[1][:, :, t].rearrange("p (i j) -> p i j", j=4),
+                in_=total[:].rearrange("p (j i) -> p i j", j=4),
+                func=ACTF.Relu,
+                bias=b1c[:, t : t + 1],
+                scale=1.0 / NODES,
+            )
+
+        acc2 = accp.tile([P, OUTF], F32, name="acc2")
+
+        def layer2(a):
+            nc.tensor.matmul_mx(
+                out=acc2[:],
+                lhsT=m1c[a][:].bitcast(FP8X4),
+                lhsT_scale=m1s[a][:],
+                rhs=w2c[:, a, :].bitcast(FP8X4),
+                rhs_scale=w2s[:, a, :],
+                start=(a == 0),
+                stop=(a == 1),
+            )
 
         w2_state = {}
 
@@ -226,101 +308,80 @@ def tile_gcn_pa_kernel(tc, x, W1g, b1g, W2g, b2g, out):
         w2c = keep.tile([P, 2, P], U32, name="w2c", align_bytes=64)
         w2s = keep.tile([P, 2, P], U8, name="w2s", align_bytes=64)
 
-        permute_w(0, 0)
-        permute_w(0, 1)
-        turn_w(0, 0, "s")
-        turn_w(0, 1, "s")
-        permute_w(0, 2)
-        permute_w(0, 3)
-        turn_w(0, 2, "s")
-        turn_w(0, 3, "s")
+        for t in range(4):
+            permute_w(0, t)
+            turn_w(0, t, "ssss"[t])
         stage_a(0)
         quant_w(0, 0)
         stage_b(0)
-        permute_w(1, 0, "v")
-        permute_w(1, 1, "v")
         quant_w(0, 1)
-        stage_c(0)
-        turn_w(1, 0, "s")
-        turn_w(1, 1, "s")
-        permute_w(1, 2, "v")
-        permute_w(1, 3, "v")
         stage_a(1)
-        passes(0, 0)
-        turn_w(1, 2, "s")
-        turn_w(1, 3, "s")
-        quant_w(1, 0)
-        stage_b(1)
-        quant_w(1, 1)
-        stage_a(2)
-        stage_c(1)
-        passes(0, 1)
-        for m in range(1, PAIRS):
+        stage_c(0)
+        for m in range(NATURAL):
+            if m + 1 < NATURAL:
+                stage_b(m + 1)
+            if m + 2 < NATURAL:
+                stage_a(m + 2)
+            if m == NATURAL - 2:
+                permute_w(1, 0)
+                permute_w(1, 1)
+            first_half(m)
+            if m + 1 < NATURAL:
+                stage_c(m + 1)
+            if m == NATURAL - 2:
+                permute_w(1, 2)
+                permute_w(1, 3)
+                for t in range(4):
+                    turn_w(1, t, "ssss"[t])
+                stage_a(NATURAL)
+                quant_w(1, 0)
+                quant_w(1, 1)
+                stage_b(NATURAL)
+                stage_a(NATURAL + 1)
+        stage_c(NATURAL)
+        def group(m):
+            for t in range(3):
+                second_half(m, t)
+            if m < 4:
+                second_half_narrow(m, 3)
+        for m in range(NATURAL):
+            group(m)
+        for m in range(NATURAL, PAIRS):
             if m + 1 < PAIRS:
                 stage_b(m + 1)
+            first_half(m)
+            if m == PAIRS - 1:
+                nc.vector.tensor_copy(out=b1c[:], in_=b1c_raw[:].rearrange("p u e -> p (u e)"))
+                mean_bias()
             if m + 2 < PAIRS:
                 stage_a(m + 2)
-            passes(m, 0)
+            if m + 1 < PAIRS:
+                stage_c(m + 1)
             if m < PAIRS - 2:
-                passes(m, 1)
+                group(m)
             if m == 6:
                 turn_w2()
-            if m + 1 < PAIRS - 1:
-                stage_c(m + 1)
-            elif m + 1 < PAIRS:
-                stage_c(m + 1, 0)
-                stage_c(m + 1, 1)
-                quant_w2()
-
-        g2 = [keep.tile([P, P, 4], BF16, name="g2%d" % a, align_bytes=64) for a in range(2)]
-        m1c = [keep.tile([P, P], U32, name="m1c%d" % a, align_bytes=64) for a in range(2)]
-        m1s = [keep.tile([P, P], U8, name="m1s%d" % a, align_bytes=64) for a in range(2)]
-
-        def mean_bias(a):
-            hid = keep.tile([P, 4, P], BF16, name="hid%d" % a)
-            nc.vector.scalar_tensor_tensor(
-                out=hid[:].rearrange("b t p -> b (t p)"),
-                in0=acc[a][:],
-                scalar=1.0 / NODES,
-                in1=b1sb[:, a, :],
-                op0=ALU.mult,
-                op1=ALU.add,
-            )
-            return hid
-
-        def turn_hidden(a, hid):
-            hid_t = tpp.tile([P, 4, P], BF16, name="hidT", tag="tp")
-            for t in range(4):
-                nc.tensor.transpose(hid_t[:, t, :], hid[:, t, :], perm_b[:])
-            nc.scalar.activation(out=g2[a][:], in_=hid_t[:].rearrange("p t b -> p b t"), func=ACTF.Relu)
-            nc.vector.quantize_mx(
-                out=m1c[a][:].bitcast(FP8X4), scales=m1s[a][:], in_=g2[a][:].rearrange("p b t -> p (b t)")
-            )
-
-        acc2 = accp.tile([P, OUTF], F32, name="acc2")
-
-        def layer2(a):
-            nc.tensor.matmul_mx(
-                out=acc2[:],
-                lhsT=m1c[a][:].bitcast(FP8X4),
-                lhsT_scale=m1s[a][:],
-                rhs=w2c[:, a, :].bitcast(FP8X4),
-                rhs_scale=w2s[:, a, :],
-                start=(a == 0),
-                stop=(a == 1),
-            )
-
-        hid0 = mean_bias(0)
-        passes(PAIRS - 2, 1)
-        turn_hidden(0, hid0)
-        passes(PAIRS - 1, 1)
-        hid1 = mean_bias(1)
+        for m in range(PAIRS - 2, PAIRS - 1):
+            for t in range(3):
+                second_half(m, t)
+        turn_hidden()
+        quant_w2()
+        second_half(PAIRS - 1, 0)
+        finish(0, True)
+        second_half(PAIRS - 1, 1)
+        finish(1, True)
+        quant_hidden(0)
+        second_half(PAIRS - 1, 2)
+        finish(2, True)
+        for m in range(4, PAIRS):
+            second_half_narrow(m, 3)
         layer2(0)
-        turn_hidden(1, hid1)
+        finish(3, False)
+        quant_hidden(1)
         layer2(1)
 
         pre = keep.tile([P, OUTF], F32, name="pre")
-        nc.vector.tensor_tensor(out=pre[:], in0=acc2[:], in1=b2sb[:], op=ALU.add)
+        nc.vector.tensor_tensor(out=pre[:], in0=acc2[:], in1=b2bc[:], op=ALU.add)
         m2r = keep.tile([P, REP, OUTF], F32, name="m2r")
         nc.vector.tensor_scalar_max(
             out=m2r[:], in0=pre[:].unsqueeze(1).to_broadcast([P, REP, OUTF]), scalar1=0.0

@@ -20,7 +20,7 @@ HID = 1024
 OUTF = 128
 FLOPS = 2 * P * NODES * FEAT * HID + 2 * P * HID * OUTF
 
-NATURAL = 2
+NATURAL = 4
 REP = 4
 WARM = 8
 
@@ -29,9 +29,10 @@ def tile_gcn_pa_kernel(tc, x, W1g, b1g, W2g, b2g, out):
     nc = tc.nc
     with ExitStack() as ctx:
         keep = ctx.enter_context(tc.tile_pool(name="keep", bufs=1))
-        stage = ctx.enter_context(tc.tile_pool(name="stage", bufs=4))
-        accp = ctx.enter_context(tc.psum_pool(name="accp", bufs=1))
-        tpp = ctx.enter_context(tc.psum_pool(name="tpp", bufs=6))
+        stage = ctx.enter_context(tc.tile_pool(name="stage", bufs=6))
+        permp = ctx.enter_context(tc.tile_pool(name="permp", bufs=16))
+        sump = ctx.enter_context(tc.psum_pool(name="sump", bufs=1))
+        tpp = ctx.enter_context(tc.psum_pool(name="tpp", bufs=4))
         ctx.enter_context(tc.manual_schedule())
 
         w1v = W1g.rearrange("(a u p e) k -> a p u e k", a=2, u=2, p=P, e=2)
@@ -40,8 +41,7 @@ def tile_gcn_pa_kernel(tc, x, W1g, b1g, W2g, b2g, out):
         w_raw = {}
         x_raw = {}
 
-        def load_w(a, t):
-            cnt = 1 if a == 0 else 2
+        def load_w(a, t, cnt):
             wt = keep.tile([P, cnt, FEAT], BF16, name="wraw%d%d" % (a, t))
             nc.sync.dma_start(out=wt[:], in_=w1v[a][:, t // 2, t % 2 : t % 2 + cnt, :])
             for e in range(cnt):
@@ -57,38 +57,36 @@ def tile_gcn_pa_kernel(tc, x, W1g, b1g, W2g, b2g, out):
                     nc.sync.dma_start(out=xt[32 * q : 32 * q + 32, :, :], in_=xq[q][:, m : 4 * NODES : 8, :])
             x_raw[m] = xt
 
-        for t in range(4):
-            load_w(0, t)
-        for m in range(2):
+        load_w(0, 0, 1)
+        load_x(0)
+        for t in range(1, 4):
+            load_w(0, t, 1)
+        for m in range(1, 4):
             load_x(m)
-        load_w(1, 0)
-        load_w(1, 2)
-        for m in range(2, PAIRS):
-            load_x(m)
+        load_w(1, 0, 2)
+        load_w(1, 2, 2)
         w2_raw = keep.tile([P, HID], BF16, name="w2_raw")
         nc.sync.dma_start(out=w2_raw[:], in_=W2g)
-        b1bc = keep.tile([P, 512], BF16, name="b1bc")
-        nc.sync.dma_start(out=b1bc[:], in_=b1g[0:512].partition_broadcast(P))
-        b1c_raw = keep.tile([P, 2, 2], BF16, name="b1c_raw")
-        nc.sync.dma_start(out=b1c_raw[:], in_=b1g[512:1024].rearrange("(u p e) -> p u e", u=2, p=P, e=2))
+        for m in range(4, PAIRS):
+            load_x(m)
+        b1c_raw = keep.tile([P, 8], BF16, name="b1c_raw")
+        nc.sync.dma_start(
+            out=b1c_raw[:].rearrange("p (v e) -> p v e", e=2), in_=b1g.rearrange("(v p e) -> p v e", v=4, p=P, e=2)
+        )
         b2bc = keep.tile([P, OUTF], BF16, name="b2bc")
         nc.sync.dma_start(out=b2bc[:], in_=b2g.partition_broadcast(P))
-        b1c = keep.tile([P, 4], F32, name="b1c")
+        b1c = keep.tile([P, 8], F32, name="b1c")
 
         zeros = keep.tile([P, 512], BF16, name="zeros")
         nc.vector.memset(zeros[:].bitcast(F32), 0.0)
         ident_f = keep.tile([P, P], F32, name="ident_f")
         make_identity(nc, ident_f[:])
-        ident_b = keep.tile([P, P], BF16, name="ident_b")
-        make_identity(nc, ident_b[:])
         warm_in = keep.tile([P, 8], F32, name="warm_in")
         warm_out = keep.tile([P, 8], F32, name="warm_out")
         nc.vector.memset(warm_in[:], 0.0)
         nc.scalar.copy(out=warm_out[:], in_=warm_in[:])
         perm_f = keep.tile([P, P], F32, name="perm_f")
         nc.scalar.copy(out=perm_f[:].rearrange("p (j i) -> p j i", j=4), in_=ident_f[:].rearrange("p (i j) -> p j i", j=4))
-        perm_b = keep.tile([P, P], BF16, name="perm_b")
-        nc.scalar.copy(out=perm_b[:].rearrange("p (i j) -> p i j", j=4), in_=ident_b[:].rearrange("p (j i) -> p i j", j=4))
 
         w1c = [keep.tile([P, 2, 512], U32, name="w1c%d" % a, align_bytes=64) for a in range(2)]
         w1s = [keep.tile([P, 2, 512], U8, name="w1s%d" % a, align_bytes=64) for a in range(2)]
@@ -98,11 +96,14 @@ def tile_gcn_pa_kernel(tc, x, W1g, b1g, W2g, b2g, out):
         for m in range(PAIRS):
             xc[m] = keep.tile([P, 2, 2, P], U32, name="xc%d" % m, align_bytes=64)
             xs[m] = keep.tile([P, 2, 2, P], U8, name="xs%d" % m, align_bytes=64)
-        acc0 = accp.tile([P, 512], F32, name="acc0")
+        sums = {}
+        for t in range(4):
+            whole_bank = sump.tile([P, 4, P], F32, name="sum0%d" % t)
+            sums[(0, t)] = whole_bank[:, 0:2, :]
 
         def keep_busy(count):
             for i in range(count):
-                nc.tensor.matmul(acc0[:], lhsT=zeros[:, 0:P], rhs=zeros[:], start=True, stop=True)
+                nc.tensor.matmul(sums[(0, 0)].rearrange("p h c -> p (h c)"), lhsT=zeros[:, 0:P], rhs=zeros[:, 0:256], start=True, stop=True)
 
         def transpose_words(words, identity):
             bank = tpp.tile([P, 4, P], F32, name="bank", tag="tp")
@@ -118,7 +119,7 @@ def tile_gcn_pa_kernel(tc, x, W1g, b1g, W2g, b2g, out):
                 nc.scalar.copy(out=dst, in_=src)
 
         def permute_words(eng, raw):
-            wp = stage.tile([P, 4, 4, 64], BF16, name="wp")
+            wp = permp.tile([P, 4, 4, 64], BF16, name="wp")
             src = raw.rearrange("p (q b k) -> p b q k", q=4, b=4)
             if eng == "v":
                 nc.vector.tensor_copy(out=wp[:], in_=src)
@@ -144,6 +145,14 @@ def tile_gcn_pa_kernel(tc, x, W1g, b1g, W2g, b2g, out):
                     in_=gw[a][:, kp * 2048 + pair * 1024 : kp * 2048 + (pair + 1) * 1024],
                 )
 
+        def quant_w_tile(a, t):
+            for kp in range(2):
+                nc.vector.quantize_mx(
+                    out=w1c[a][:, kp, t * P : (t + 1) * P].bitcast(FP8X4),
+                    scales=w1s[a][:, kp, t * P : (t + 1) * P],
+                    in_=gw[a][:, kp * 2048 + t * 512 : kp * 2048 + (t + 1) * 512],
+                )
+
         def quant_w_whole(a):
             for kp in range(2):
                 nc.vector.quantize_mx(
@@ -163,14 +172,14 @@ def tile_gcn_pa_kernel(tc, x, W1g, b1g, W2g, b2g, out):
                 nc.vector.transpose(out=xt[:], in_=x_raw[m][:].rearrange("p r k -> p (r k)").bitcast(F32))
                 x_words[m] = xt
 
-        def stage_b(m):
+        def stage_b(m, engs="ss"):
             gx = stage.tile([P, 2, 2, 512], BF16, name="gx", align_bytes=64)
             x_g[m] = gx
             for h in range(2):
                 if m < NATURAL:
                     bank = transpose_words(x_words[m][h], perm_f)
                     dst = gx[:].rearrange("p k h w -> p (k h w)").bitcast(F32).rearrange("p (k h c u) -> p h k c u", k=2, h=2, u=2)
-                    copy_out("s", dst[:, h, :, :, :], bank)
+                    copy_out(engs[h], dst[:, h, :, :, :], bank)
                 else:
                     src = x_words[m][:].rearrange("p (j h u k i) -> p h k j i u", j=4, h=2, u=2, k=2, i=32)
                     for kp in range(2):
@@ -184,101 +193,68 @@ def tile_gcn_pa_kernel(tc, x, W1g, b1g, W2g, b2g, out):
                 in_=x_g[m][:].rearrange("p k h w -> p (k h w)"),
             )
 
-        def first_half(m):
-            for h in range(2):
-                for kp in range(2):
-                    nc.tensor.matmul_mx(
-                        out=acc0[:],
-                        lhsT=xc[m][:, kp, h, :].bitcast(FP8X4),
-                        lhsT_scale=xs[m][:, kp, h, :],
-                        rhs=w1c[0][:, kp, :].bitcast(FP8X4),
-                        rhs_scale=w1s[0][:, kp, :],
-                        start=(m == 0 and h == 0 and kp == 0),
-                        stop=(m == PAIRS - 1 and h == 1 and kp == 1),
-                    )
-
-        sums = {}
-
-        def second_half(m, t):
-            if m == 0:
-                sums[t] = tpp.tile([P, 2, P], F32, name="sum", tag="tp")
+        def passes(m, a, t):
+            if m == 0 and a == 1:
+                whole_bank = tpp.tile([P, 4, P], F32, name="sum1", tag="tp")
+                sums[(a, t)] = whole_bank[:, 0:2, :]
             for kp in range(2):
                 nc.tensor.matmul_mx(
-                    out=sums[t][:].rearrange("p s b -> p (s b)"),
-                    lhsT=w1c[1][:, kp, t * P : (t + 1) * P].bitcast(FP8X4),
-                    lhsT_scale=w1s[1][:, kp, t * P : (t + 1) * P],
-                    rhs=xc[m][:, kp, :, :].rearrange("p s b -> p (s b)").bitcast(FP8X4),
-                    rhs_scale=xs[m][:, kp, :, :].rearrange("p s b -> p (s b)"),
+                    out=sums[(a, t)].rearrange("p h c -> p (h c)"),
+                    lhsT=w1c[a][:, kp, t * P : (t + 1) * P].bitcast(FP8X4),
+                    lhsT_scale=w1s[a][:, kp, t * P : (t + 1) * P],
+                    rhs=xc[m][:, kp, :, :].rearrange("p h c -> p (h c)").bitcast(FP8X4),
+                    rhs_scale=xs[m][:, kp, :, :].rearrange("p h c -> p (h c)"),
                     start=(m == 0 and kp == 0),
                     stop=(m == PAIRS - 1 and kp == 1),
                 )
 
-        def second_half_narrow(m, t):
-            if m == 0:
-                sums[t] = tpp.tile([P, P], F32, name="sum", tag="tp")
+        def passes_narrow(m, a, t):
+            if m == 0 and a == 1:
+                whole_bank = tpp.tile([P, 4, P], F32, name="sum1", tag="tp")
+                sums[(a, t)] = whole_bank[:, 0, :]
             for h in range(2):
                 for kp in range(2):
                     nc.tensor.matmul_mx(
-                        out=sums[t][:],
-                        lhsT=w1c[1][:, kp, t * P : (t + 1) * P].bitcast(FP8X4),
-                        lhsT_scale=w1s[1][:, kp, t * P : (t + 1) * P],
+                        out=sums[(a, t)],
+                        lhsT=w1c[a][:, kp, t * P : (t + 1) * P].bitcast(FP8X4),
+                        lhsT_scale=w1s[a][:, kp, t * P : (t + 1) * P],
                         rhs=xc[m][:, kp, h, :].bitcast(FP8X4),
                         rhs_scale=xs[m][:, kp, h, :],
                         start=(m == 0 and h == 0 and kp == 0),
                         stop=(m == PAIRS - 1 and h == 1 and kp == 1),
                     )
 
-        keep_busy(WARM)
+        keep_busy(2 * WARM)
 
         g2 = [keep.tile([P, P, 4], BF16, name="g2%d" % a, align_bytes=64) for a in range(2)]
         m1c = [keep.tile([P, P], U32, name="m1c%d" % a, align_bytes=64) for a in range(2)]
         m1s = [keep.tile([P, P], U8, name="m1s%d" % a, align_bytes=64) for a in range(2)]
-        hid0 = keep.tile([P, 4, P], BF16, name="hid0")
-        b1v = b1bc[:].rearrange("b (u p e) -> b u e p", u=2, p=P, e=2)
-
-        def mean_bias():
-            for u in range(2):
-                nc.vector.scalar_tensor_tensor(
-                    out=hid0[:, 2 * u : 2 * u + 2, :],
-                    in0=acc0[:].rearrange("b (t p) -> b t p", t=4)[:, 2 * u : 2 * u + 2, :],
-                    scalar=1.0 / NODES,
-                    in1=b1v[:, u, :, :],
-                    op0=ALU.mult,
-                    op1=ALU.add,
-                )
-
-        def turn_hidden():
-            hid_t = tpp.tile([P, 4, P], BF16, name="hidT", tag="tp")
-            for t in range(4):
-                nc.tensor.transpose(hid_t[:, t, :], hid0[:, t, :], perm_b[:])
-            nc.scalar.activation(out=g2[0][:], in_=hid_t[:].rearrange("p t b -> p b t"), func=ACTF.Relu)
 
         def quant_hidden(a):
             nc.vector.quantize_mx(
                 out=m1c[a][:].bitcast(FP8X4), scales=m1s[a][:], in_=g2[a][:].rearrange("p b t -> p (b t)")
             )
 
-        def finish(t, wide):
+        def finish(a, t, wide):
             if wide:
                 total = stage.tile([P, P], F32, name="total")
                 nc.vector.tensor_reduce(
-                    out=total[:], in_=sums[t][:].rearrange("p s b -> p b s"), axis=AXIS_X, op=ALU.add
+                    out=total[:], in_=sums[(a, t)].rearrange("p h c -> p c h"), axis=AXIS_X, op=ALU.add
                 )
+                total = total[:]
             else:
-                total = sums[t]
+                total = sums[(a, t)]
             nc.scalar.activation(
-                out=g2[1][:, :, t].rearrange("p (i j) -> p i j", j=4),
-                in_=total[:].rearrange("p (j i) -> p i j", j=4),
+                out=g2[a][:, :, t].rearrange("p (i j) -> p i j", j=4),
+                in_=total.rearrange("p (j i) -> p i j", j=4),
                 func=ACTF.Relu,
-                bias=b1c[:, t : t + 1],
+                bias=b1c[:, 4 * a + t : 4 * a + t + 1],
                 scale=1.0 / NODES,
             )
 
-        acc2 = accp.tile([P, OUTF], F32, name="acc2")
-
-        def layer2(a):
+        def layer2(acc2, a):
             nc.tensor.matmul_mx(
-                out=acc2[:],
+                out=acc2,
                 lhsT=m1c[a][:].bitcast(FP8X4),
                 lhsT_scale=m1s[a][:],
                 rhs=w2c[:, a, :].bitcast(FP8X4),
@@ -308,80 +284,89 @@ def tile_gcn_pa_kernel(tc, x, W1g, b1g, W2g, b2g, out):
         w2c = keep.tile([P, 2, P], U32, name="w2c", align_bytes=64)
         w2s = keep.tile([P, 2, P], U8, name="w2s", align_bytes=64)
 
-        for t in range(4):
-            permute_w(0, t)
-            turn_w(0, t, "ssss"[t])
+        permute_w(0, 0)
         stage_a(0)
-        quant_w(0, 0)
-        stage_b(0)
-        quant_w(0, 1)
+        permute_w(0, 1)
+        turn_w(0, 0, "s")
+        permute_w(0, 2)
+        quant_w_tile(0, 0)
+        permute_w(0, 3)
+        stage_b(0, "sv")
+        turn_w(0, 1, "s")
         stage_a(1)
         stage_c(0)
-        for m in range(NATURAL):
-            if m + 1 < NATURAL:
-                stage_b(m + 1)
-            if m + 2 < NATURAL:
-                stage_a(m + 2)
-            if m == NATURAL - 2:
-                permute_w(1, 0)
-                permute_w(1, 1)
-            first_half(m)
-            if m + 1 < NATURAL:
-                stage_c(m + 1)
-            if m == NATURAL - 2:
-                permute_w(1, 2)
-                permute_w(1, 3)
-                for t in range(4):
-                    turn_w(1, t, "ssss"[t])
-                stage_a(NATURAL)
-                quant_w(1, 0)
-                quant_w(1, 1)
-                stage_b(NATURAL)
-                stage_a(NATURAL + 1)
-        stage_c(NATURAL)
-        def group(m):
+        turn_w(0, 2, "s")
+        stage_a(2)
+        turn_w(0, 3, "s")
+        quant_w_tile(0, 1)
+        stage_b(1)
+        passes(0, 0, 0)
+        stage_a(3)
+        stage_b(2)
+        stage_c(1)
+        stage_b(3)
+        for t in range(2, 4):
+            quant_w_tile(0, t)
+        for t in range(4):
+            permute_w(1, t)
+        passes(0, 0, 1)
+        passes(1, 0, 0)
+        passes(1, 0, 1)
+        for t in range(4):
+            turn_w(1, t, "s")
+        turn_w2()
+        stage_c(2)
+        stage_c(3)
+        for t in range(2, 4):
+            for m in range(2):
+                passes(m, 0, t)
+        quant_w(1, 0)
+        stage_a(4)
+        stage_b(4)
+        quant_w(1, 1)
+        stage_a(5)
+        for m in range(2, 4):
+            for t in range(4):
+                passes(m, 0, t)
+        stage_b(5)
+        stage_c(4)
+        quant_w2()
+        def second(m):
             for t in range(3):
-                second_half(m, t)
+                passes(m, 1, t)
             if m < 4:
-                second_half_narrow(m, 3)
-        for m in range(NATURAL):
-            group(m)
-        for m in range(NATURAL, PAIRS):
-            if m + 1 < PAIRS:
-                stage_b(m + 1)
-            first_half(m)
-            if m == PAIRS - 1:
-                nc.vector.tensor_copy(out=b1c[:], in_=b1c_raw[:].rearrange("p u e -> p (u e)"))
-                mean_bias()
+                passes_narrow(m, 1, 3)
+        for m in range(4):
+            second(m)
+        for m in range(4, PAIRS):
             if m + 2 < PAIRS:
                 stage_a(m + 2)
+                stage_b(m + 2)
             if m + 1 < PAIRS:
                 stage_c(m + 1)
+            for t in range(4):
+                passes(m, 0, t)
             if m < PAIRS - 2:
-                group(m)
-            if m == 6:
-                turn_w2()
-        for m in range(PAIRS - 2, PAIRS - 1):
-            for t in range(3):
-                second_half(m, t)
-        turn_hidden()
-        quant_w2()
-        second_half(PAIRS - 1, 0)
-        finish(0, True)
-        second_half(PAIRS - 1, 1)
-        finish(1, True)
+                second(m)
+        nc.vector.tensor_copy(out=b1c[:], in_=b1c_raw[:])
+        for t in range(4):
+            finish(0, t, True)
         quant_hidden(0)
-        second_half(PAIRS - 1, 2)
-        finish(2, True)
+        for t in range(3):
+            for m in range(PAIRS - 2, PAIRS):
+                passes(m, 1, t)
+            finish(1, t, True)
         for m in range(4, PAIRS):
-            second_half_narrow(m, 3)
-        layer2(0)
-        finish(3, False)
+            passes_narrow(m, 1, 3)
+        acc2_bank = sump.tile([P, 4, P], F32, name="sum00")
+        acc2 = acc2_bank[:, 0, :]
+        layer2(acc2, 0)
+        finish(1, 3, False)
         quant_hidden(1)
-        layer2(1)
+        layer2(acc2, 1)
 
         pre = keep.tile([P, OUTF], F32, name="pre")
-        nc.vector.tensor_tensor(out=pre[:], in0=acc2[:], in1=b2bc[:], op=ALU.add)
+        nc.vector.tensor_tensor(out=pre[:], in0=acc2, in1=b2bc[:], op=ALU.add)
         m2r = keep.tile([P, REP, OUTF], F32, name="m2r")
         nc.vector.tensor_scalar_max(
             out=m2r[:], in0=pre[:].unsqueeze(1).to_broadcast([P, REP, OUTF]), scalar1=0.0

@@ -30,9 +30,9 @@ def tile_gcn_pa_kernel(tc, x, W1g, b1g, W2g, b2g, out):
     with ExitStack() as ctx:
         keep = ctx.enter_context(tc.tile_pool(name="keep", bufs=1))
         stage = ctx.enter_context(tc.tile_pool(name="stage", bufs=6))
-        permp = ctx.enter_context(tc.tile_pool(name="permp", bufs=16))
-        sump = ctx.enter_context(tc.psum_pool(name="sump", bufs=1))
-        tpp = ctx.enter_context(tc.psum_pool(name="tpp", bufs=4))
+        permp = ctx.enter_context(tc.tile_pool(name="permp", bufs=6))
+        accp = ctx.enter_context(tc.psum_pool(name="accp", bufs=1))
+        tpp = ctx.enter_context(tc.psum_pool(name="tpp", bufs=6))
         ctx.enter_context(tc.manual_schedule())
 
         w1v = W1g.rearrange("(a u p e) k -> a p u e k", a=2, u=2, p=P, e=2)
@@ -44,8 +44,7 @@ def tile_gcn_pa_kernel(tc, x, W1g, b1g, W2g, b2g, out):
         def load_w(a, t, cnt):
             wt = keep.tile([P, cnt, FEAT], BF16, name="wraw%d%d" % (a, t))
             nc.sync.dma_start(out=wt[:], in_=w1v[a][:, t // 2, t % 2 : t % 2 + cnt, :])
-            for e in range(cnt):
-                w_raw[(a, t + e)] = wt[:, e, :]
+            w_raw[(a, t)] = (wt, cnt)
 
         def load_x(m):
             if m < NATURAL:
@@ -69,41 +68,42 @@ def tile_gcn_pa_kernel(tc, x, W1g, b1g, W2g, b2g, out):
         nc.sync.dma_start(out=w2_raw[:], in_=W2g)
         for m in range(4, PAIRS):
             load_x(m)
-        b1c_raw = keep.tile([P, 8], BF16, name="b1c_raw")
-        nc.sync.dma_start(
-            out=b1c_raw[:].rearrange("p (v e) -> p v e", e=2), in_=b1g.rearrange("(v p e) -> p v e", v=4, p=P, e=2)
-        )
         b2bc = keep.tile([P, OUTF], BF16, name="b2bc")
         nc.sync.dma_start(out=b2bc[:], in_=b2g.partition_broadcast(P))
-        b1c = keep.tile([P, 8], F32, name="b1c")
+        b1bc = keep.tile([P, 512], BF16, name="b1bc")
+        nc.sync.dma_start(out=b1bc[:], in_=b1g[0:512].partition_broadcast(P))
+        b1c_raw = keep.tile([P, 2, 2], BF16, name="b1c_raw")
+        nc.sync.dma_start(out=b1c_raw[:], in_=b1g[512:1024].rearrange("(u p e) -> p u e", u=2, p=P, e=2))
+        b1c = keep.tile([P, 4], F32, name="b1c")
 
         zeros = keep.tile([P, 512], BF16, name="zeros")
         nc.vector.memset(zeros[:].bitcast(F32), 0.0)
         ident_f = keep.tile([P, P], F32, name="ident_f")
         make_identity(nc, ident_f[:])
+        ident_b = keep.tile([P, P], BF16, name="ident_b")
+        make_identity(nc, ident_b[:])
         warm_in = keep.tile([P, 8], F32, name="warm_in")
         warm_out = keep.tile([P, 8], F32, name="warm_out")
         nc.vector.memset(warm_in[:], 0.0)
         nc.scalar.copy(out=warm_out[:], in_=warm_in[:])
         perm_f = keep.tile([P, P], F32, name="perm_f")
         nc.scalar.copy(out=perm_f[:].rearrange("p (j i) -> p j i", j=4), in_=ident_f[:].rearrange("p (i j) -> p j i", j=4))
+        perm_b = keep.tile([P, P], BF16, name="perm_b")
+        nc.scalar.copy(out=perm_b[:].rearrange("p (i j) -> p i j", j=4), in_=ident_b[:].rearrange("p (j i) -> p i j", j=4))
 
         w1c = [keep.tile([P, 2, 512], U32, name="w1c%d" % a, align_bytes=64) for a in range(2)]
         w1s = [keep.tile([P, 2, 512], U8, name="w1s%d" % a, align_bytes=64) for a in range(2)]
         gw = [keep.tile([P, 4096], BF16, name="gw%d" % a, align_bytes=64) for a in range(2)]
         xc = {}
         xs = {}
-        for m in range(PAIRS):
-            xc[m] = keep.tile([P, 2, 2, P], U32, name="xc%d" % m, align_bytes=64)
-            xs[m] = keep.tile([P, 2, 2, P], U8, name="xs%d" % m, align_bytes=64)
-        sums = {}
-        for t in range(4):
-            whole_bank = sump.tile([P, 4, P], F32, name="sum0%d" % t)
-            sums[(0, t)] = whole_bank[:, 0:2, :]
+        for g in range(PAIRS // 2):
+            xc[g] = keep.tile([P, 2, 4, P], U32, name="xc%d" % g, align_bytes=64)
+            xs[g] = keep.tile([P, 2, 4, P], U8, name="xs%d" % g, align_bytes=64)
+        acc0 = accp.tile([P, 512], F32, name="acc0")
 
         def keep_busy(count):
             for i in range(count):
-                nc.tensor.matmul(sums[(0, 0)].rearrange("p h c -> p (h c)"), lhsT=zeros[:, 0:P], rhs=zeros[:, 0:256], start=True, stop=True)
+                nc.tensor.matmul(acc0[:], lhsT=zeros[:, 0:P], rhs=zeros[:], start=True, stop=True)
 
         def transpose_words(words, identity):
             bank = tpp.tile([P, 4, P], F32, name="bank", tag="tp")
@@ -118,19 +118,19 @@ def tile_gcn_pa_kernel(tc, x, W1g, b1g, W2g, b2g, out):
             else:
                 nc.scalar.copy(out=dst, in_=src)
 
-        def permute_words(eng, raw):
-            wp = permp.tile([P, 4, 4, 64], BF16, name="wp")
-            src = raw.rearrange("p (q b k) -> p b q k", q=4, b=4)
-            if eng == "v":
-                nc.vector.tensor_copy(out=wp[:], in_=src)
-            else:
-                nc.scalar.copy(out=wp[:], in_=src)
-            return wp[:].rearrange("p b q k -> p (b q k)").bitcast(F32)
+        def permute_words(raw, rows):
+            wp = permp.tile([P, rows, 4, 4, 64], BF16, name="wp%d" % rows)
+            nc.vector.tensor_copy(out=wp[:], in_=raw.rearrange("p h (q b k) -> p h b q k", q=4, b=4))
+            words = wp[:].rearrange("p h b q k -> p h (b q k)").bitcast(F32)
+            return [words[:, h, :] for h in range(rows)]
 
         w_words = {}
 
-        def permute_w(a, t, eng="v"):
-            w_words[(a, t)] = permute_words(eng, w_raw[(a, t)])
+        def permute_w(a, t):
+            raw, cnt = w_raw[(a, t)]
+            words = permute_words(raw[:], cnt)
+            for e in range(cnt):
+                w_words[(a, t + e)] = words[e]
 
         def turn_w(a, t, eng):
             bank = transpose_words(w_words[(a, t)], ident_f)
@@ -153,20 +153,12 @@ def tile_gcn_pa_kernel(tc, x, W1g, b1g, W2g, b2g, out):
                     in_=gw[a][:, kp * 2048 + t * 512 : kp * 2048 + (t + 1) * 512],
                 )
 
-        def quant_w_whole(a):
-            for kp in range(2):
-                nc.vector.quantize_mx(
-                    out=w1c[a][:, kp, :].bitcast(FP8X4),
-                    scales=w1s[a][:, kp, :],
-                    in_=gw[a][:, kp * 2048 : (kp + 1) * 2048],
-                )
-
         x_words = {}
         x_g = {}
 
-        def stage_a(m, eng="v"):
+        def stage_a(m):
             if m < NATURAL:
-                x_words[m] = [permute_words(eng, x_raw[m][:, h, :]) for h in range(2)]
+                x_words[m] = permute_words(x_raw[m][:], 2)
             else:
                 xt = stage.tile([P, 1024], F32, name="xt", align_bytes=64)
                 nc.vector.transpose(out=xt[:], in_=x_raw[m][:].rearrange("p r k -> p (r k)").bitcast(F32))
@@ -175,86 +167,124 @@ def tile_gcn_pa_kernel(tc, x, W1g, b1g, W2g, b2g, out):
         def stage_b(m, engs="ss"):
             gx = stage.tile([P, 2, 2, 512], BF16, name="gx", align_bytes=64)
             x_g[m] = gx
-            for h in range(2):
-                if m < NATURAL:
-                    bank = transpose_words(x_words[m][h], perm_f)
-                    dst = gx[:].rearrange("p k h w -> p (k h w)").bitcast(F32).rearrange("p (k h c u) -> p h k c u", k=2, h=2, u=2)
-                    copy_out(engs[h], dst[:, h, :, :, :], bank)
-                else:
-                    src = x_words[m][:].rearrange("p (j h u k i) -> p h k j i u", j=4, h=2, u=2, k=2, i=32)
-                    for kp in range(2):
-                        dst = gx[:, kp, h, :].bitcast(F32).rearrange("p (j i u) -> p j i u", j=4, i=32, u=2)
-                        nc.scalar.copy(out=dst, in_=src[:, h, kp, :, :, :])
+            if m < NATURAL:
+                dst = gx[:].rearrange("p k h w -> p (k h w)").bitcast(F32).rearrange("p (k h c u) -> p h k c u", k=2, h=2, u=2)
+                for h in range(2):
+                    copy_out(engs[h], dst[:, h, :, :, :], transpose_words(x_words[m][h], perm_f))
+            else:
+                src = x_words[m][:].rearrange("p (j h u k i) -> p k h j i u", j=4, h=2, u=2, k=2, i=32)
+                for kp in range(2):
+                    dst = gx[:, kp, :, :].rearrange("p h w -> p (h w)").bitcast(F32)
+                    nc.scalar.copy(
+                        out=dst.rearrange("p (h j i u) -> p h j i u", h=2, j=4, i=32, u=2), in_=src[:, kp, :, :, :, :]
+                    )
 
         def stage_c(m):
-            nc.vector.quantize_mx(
-                out=xc[m][:].rearrange("p k n c -> p (k n c)").bitcast(FP8X4),
-                scales=xs[m][:].rearrange("p k n c -> p (k n c)"),
-                in_=x_g[m][:].rearrange("p k h w -> p (k h w)"),
-            )
-
-        def passes(m, a, t):
-            if m == 0 and a == 1:
-                whole_bank = tpp.tile([P, 4, P], F32, name="sum1", tag="tp")
-                sums[(a, t)] = whole_bank[:, 0:2, :]
+            s = 2 * (m % 2)
             for kp in range(2):
-                nc.tensor.matmul_mx(
-                    out=sums[(a, t)].rearrange("p h c -> p (h c)"),
-                    lhsT=w1c[a][:, kp, t * P : (t + 1) * P].bitcast(FP8X4),
-                    lhsT_scale=w1s[a][:, kp, t * P : (t + 1) * P],
-                    rhs=xc[m][:, kp, :, :].rearrange("p h c -> p (h c)").bitcast(FP8X4),
-                    rhs_scale=xs[m][:, kp, :, :].rearrange("p h c -> p (h c)"),
-                    start=(m == 0 and kp == 0),
-                    stop=(m == PAIRS - 1 and kp == 1),
+                nc.vector.quantize_mx(
+                    out=xc[m // 2][:, kp, s : s + 2, :].rearrange("p n c -> p (n c)").bitcast(FP8X4),
+                    scales=xs[m // 2][:, kp, s : s + 2, :].rearrange("p n c -> p (n c)"),
+                    in_=x_g[m][:, kp, :, :].rearrange("p h w -> p (h w)"),
                 )
 
-        def passes_narrow(m, a, t):
-            if m == 0 and a == 1:
-                whole_bank = tpp.tile([P, 4, P], F32, name="sum1", tag="tp")
-                sums[(a, t)] = whole_bank[:, 0, :]
+        def first_half(m):
             for h in range(2):
+                n = 2 * (m % 2) + h
                 for kp in range(2):
                     nc.tensor.matmul_mx(
-                        out=sums[(a, t)],
-                        lhsT=w1c[a][:, kp, t * P : (t + 1) * P].bitcast(FP8X4),
-                        lhsT_scale=w1s[a][:, kp, t * P : (t + 1) * P],
-                        rhs=xc[m][:, kp, h, :].bitcast(FP8X4),
-                        rhs_scale=xs[m][:, kp, h, :],
+                        out=acc0[:],
+                        lhsT=xc[m // 2][:, kp, n, :].bitcast(FP8X4),
+                        lhsT_scale=xs[m // 2][:, kp, n, :],
+                        rhs=w1c[0][:, kp, :].bitcast(FP8X4),
+                        rhs_scale=w1s[0][:, kp, :],
                         start=(m == 0 and h == 0 and kp == 0),
                         stop=(m == PAIRS - 1 and h == 1 and kp == 1),
                     )
 
-        keep_busy(2 * WARM)
+        sums = {}
+
+        def second_half(g, t):
+            if g == 0:
+                sums[t] = tpp.tile([P, 4, P], F32, name="sum", tag="tp")
+            for kp in range(2):
+                nc.tensor.matmul_mx(
+                    out=sums[t][:].rearrange("p s b -> p (s b)"),
+                    lhsT=w1c[1][:, kp, t * P : (t + 1) * P].bitcast(FP8X4),
+                    lhsT_scale=w1s[1][:, kp, t * P : (t + 1) * P],
+                    rhs=xc[g][:, kp, :, :].rearrange("p s b -> p (s b)").bitcast(FP8X4),
+                    rhs_scale=xs[g][:, kp, :, :].rearrange("p s b -> p (s b)"),
+                    start=(g == 0 and kp == 0),
+                    stop=(g == 3 and kp == 1),
+                )
+
+        def second_half_narrow(g, t):
+            if g == 0:
+                sums[t] = tpp.tile([P, 4, P], F32, name="sum", tag="tp")
+            for n in range(4):
+                for kp in range(2):
+                    nc.tensor.matmul_mx(
+                        out=sums[t][:, 0, :],
+                        lhsT=w1c[1][:, kp, t * P : (t + 1) * P].bitcast(FP8X4),
+                        lhsT_scale=w1s[1][:, kp, t * P : (t + 1) * P],
+                        rhs=xc[g][:, kp, n, :].bitcast(FP8X4),
+                        rhs_scale=xs[g][:, kp, n, :],
+                        start=(g == 0 and n == 0 and kp == 0),
+                        stop=(g == 3 and n == 3 and kp == 1),
+                    )
+
+        keep_busy(WARM)
 
         g2 = [keep.tile([P, P, 4], BF16, name="g2%d" % a, align_bytes=64) for a in range(2)]
         m1c = [keep.tile([P, P], U32, name="m1c%d" % a, align_bytes=64) for a in range(2)]
         m1s = [keep.tile([P, P], U8, name="m1s%d" % a, align_bytes=64) for a in range(2)]
+        hid0 = keep.tile([P, 4, P], BF16, name="hid0")
+        b1v = b1bc[:].rearrange("b (u p e) -> b u e p", u=2, p=P, e=2)
+
+        def mean_bias():
+            for u in range(2):
+                nc.vector.scalar_tensor_tensor(
+                    out=hid0[:, 2 * u : 2 * u + 2, :],
+                    in0=acc0[:].rearrange("b (t p) -> b t p", t=4)[:, 2 * u : 2 * u + 2, :],
+                    scalar=1.0 / NODES,
+                    in1=b1v[:, u, :, :],
+                    op0=ALU.mult,
+                    op1=ALU.add,
+                )
+
+        def turn_hidden():
+            hid_t = tpp.tile([P, 4, P], BF16, name="hidT", tag="tp")
+            for t in range(4):
+                nc.tensor.transpose(hid_t[:, t, :], hid0[:, t, :], perm_b[:])
+            nc.scalar.activation(out=g2[0][:], in_=hid_t[:].rearrange("p t b -> p b t"), func=ACTF.Relu)
 
         def quant_hidden(a):
             nc.vector.quantize_mx(
                 out=m1c[a][:].bitcast(FP8X4), scales=m1s[a][:], in_=g2[a][:].rearrange("p b t -> p (b t)")
             )
 
-        def finish(a, t, wide):
+        def finish(t, wide):
             if wide:
                 total = stage.tile([P, P], F32, name="total")
                 nc.vector.tensor_reduce(
-                    out=total[:], in_=sums[(a, t)].rearrange("p h c -> p c h"), axis=AXIS_X, op=ALU.add
+                    out=total[:], in_=sums[t][:].rearrange("p s b -> p b s"), axis=AXIS_X, op=ALU.add
                 )
                 total = total[:]
             else:
-                total = sums[(a, t)]
+                total = sums[t][:, 0, :]
             nc.scalar.activation(
-                out=g2[a][:, :, t].rearrange("p (i j) -> p i j", j=4),
+                out=g2[1][:, :, t].rearrange("p (i j) -> p i j", j=4),
                 in_=total.rearrange("p (j i) -> p i j", j=4),
                 func=ACTF.Relu,
-                bias=b1c[:, 4 * a + t : 4 * a + t + 1],
+                bias=b1c[:, t : t + 1],
                 scale=1.0 / NODES,
             )
 
-        def layer2(acc2, a):
+        acc2 = accp.tile([P, OUTF], F32, name="acc2")
+
+        def layer2(a):
             nc.tensor.matmul_mx(
-                out=acc2,
+                out=acc2[:],
                 lhsT=m1c[a][:].bitcast(FP8X4),
                 lhsT_scale=m1s[a][:],
                 rhs=w2c[:, a, :].bitcast(FP8X4),
@@ -300,73 +330,69 @@ def tile_gcn_pa_kernel(tc, x, W1g, b1g, W2g, b2g, out):
         turn_w(0, 3, "s")
         quant_w_tile(0, 1)
         stage_b(1)
-        passes(0, 0, 0)
         stage_a(3)
         stage_b(2)
+        quant_w_tile(0, 2)
+        quant_w_tile(0, 3)
         stage_c(1)
         stage_b(3)
-        for t in range(2, 4):
-            quant_w_tile(0, t)
-        for t in range(4):
-            permute_w(1, t)
-        passes(0, 0, 1)
-        passes(1, 0, 0)
-        passes(1, 0, 1)
+        first_half(0)
+        permute_w(1, 0)
+        permute_w(1, 2)
+        first_half(1)
         for t in range(4):
             turn_w(1, t, "s")
         turn_w2()
         stage_c(2)
         stage_c(3)
-        for t in range(2, 4):
-            for m in range(2):
-                passes(m, 0, t)
+        first_half(2)
         quant_w(1, 0)
         stage_a(4)
         stage_b(4)
         quant_w(1, 1)
         stage_a(5)
-        for m in range(2, 4):
-            for t in range(4):
-                passes(m, 0, t)
+        first_half(3)
         stage_b(5)
         stage_c(4)
         quant_w2()
-        def second(m):
+        def second(g):
             for t in range(3):
-                passes(m, 1, t)
-            if m < 4:
-                passes_narrow(m, 1, 3)
-        for m in range(4):
-            second(m)
-        for m in range(4, PAIRS):
-            if m + 2 < PAIRS:
-                stage_a(m + 2)
-                stage_b(m + 2)
-            if m + 1 < PAIRS:
-                stage_c(m + 1)
-            for t in range(4):
-                passes(m, 0, t)
-            if m < PAIRS - 2:
-                second(m)
-        nc.vector.tensor_copy(out=b1c[:], in_=b1c_raw[:])
-        for t in range(4):
-            finish(0, t, True)
+                second_half(g, t)
+            if g < 2:
+                second_half_narrow(g, 3)
+        for g in range(2):
+            second(g)
+        stage_a(6)
+        stage_b(6)
+        first_half(4)
+        stage_c(5)
+        first_half(5)
+        stage_a(7)
+        stage_b(7)
+        stage_c(6)
+        second(2)
+        first_half(6)
+        stage_c(7)
+        first_half(7)
+        nc.vector.tensor_copy(out=b1c[:], in_=b1c_raw[:].rearrange("p u e -> p (u e)"))
+        mean_bias()
+        second_half(3, 0)
+        finish(0, True)
+        second_half(3, 1)
+        turn_hidden()
+        finish(1, True)
+        second_half(3, 2)
+        finish(2, True)
+        for g in range(2, 4):
+            second_half_narrow(g, 3)
         quant_hidden(0)
-        for t in range(3):
-            for m in range(PAIRS - 2, PAIRS):
-                passes(m, 1, t)
-            finish(1, t, True)
-        for m in range(4, PAIRS):
-            passes_narrow(m, 1, 3)
-        acc2_bank = sump.tile([P, 4, P], F32, name="sum00")
-        acc2 = acc2_bank[:, 0, :]
-        layer2(acc2, 0)
-        finish(1, 3, False)
+        layer2(0)
+        finish(3, False)
         quant_hidden(1)
-        layer2(acc2, 1)
+        layer2(1)
 
         pre = keep.tile([P, OUTF], F32, name="pre")
-        nc.vector.tensor_tensor(out=pre[:], in0=acc2, in1=b2bc[:], op=ALU.add)
+        nc.vector.tensor_tensor(out=pre[:], in0=acc2[:], in1=b2bc[:], op=ALU.add)
         m2r = keep.tile([P, REP, OUTF], F32, name="m2r")
         nc.vector.tensor_scalar_max(
             out=m2r[:], in0=pre[:].unsqueeze(1).to_broadcast([P, REP, OUTF]), scalar1=0.0

from contextlib import ExitStack

import concourse.mybir as mybir
from concourse.masks import make_identity

F32 = mybir.dt.float32
BF16 = mybir.dt.bfloat16
U32 = mybir.dt.uint32
U8 = mybir.dt.uint8
FP8X4 = mybir.dt.float8_e4m3fn_x4
ALU = mybir.AluOpType
ACTF = mybir.ActivationFunctionType
AXIS_X = mybir.AxisListType.X

P = 128
NODES = 16
PAIRS = 8
FEAT = 1024
HID = 1024
OUTF = 128
FLOPS = 2 * P * NODES * FEAT * HID + 2 * P * HID * OUTF

NATURAL = 4
REP = 4
WARM = 8


def tile_gcn_pa_kernel(tc, x, W1g, b1g, W2g, b2g, out):
    nc = tc.nc
    with ExitStack() as ctx:
        keep = ctx.enter_context(tc.tile_pool(name="keep", bufs=1))
        stage = ctx.enter_context(tc.tile_pool(name="stage", bufs=6))
        permp = ctx.enter_context(tc.tile_pool(name="permp", bufs=6))
        accp = ctx.enter_context(tc.psum_pool(name="accp", bufs=1))
        tpp = ctx.enter_context(tc.psum_pool(name="tpp", bufs=6))
        ctx.enter_context(tc.manual_schedule())

        w1v = W1g.rearrange("(a u p e) k -> a p u e k", a=2, u=2, p=P, e=2)
        xq = x.rearrange("(i j) c h (q k) -> q i (j c h) k", i=32, j=4, q=4)
        xn = x.rearrange("b c h f -> b (c h) f")
        w_raw = {}
        x_raw = {}

        def load_w(a, t, cnt):
            wt = keep.tile([P, cnt, FEAT], BF16, name="wraw%d%d" % (a, t))
            nc.sync.dma_start(out=wt[:], in_=w1v[a][:, t // 2, t % 2 : t % 2 + cnt, :])
            w_raw[(a, t)] = (wt, cnt)

        def load_x(m):
            if m < NATURAL:
                xt = keep.tile([P, 2, FEAT], BF16, name="xraw%d" % m)
                nc.sync.dma_start(out=xt[:], in_=xn[:, m:NODES:8, :])
            else:
                xt = keep.tile([P, 8, 256], BF16, name="xraw%d" % m, align_bytes=64)
                for q in (0, 2, 1, 3):
                    nc.sync.dma_start(out=xt[32 * q : 32 * q + 32, :, :], in_=xq[q][:, m : 4 * NODES : 8, :])
            x_raw[m] = xt

        load_w(0, 0, 1)
        load_x(0)
        for t in range(1, 4):
            load_w(0, t, 1)
        for m in range(1, 4):
            load_x(m)
        load_w(1, 0, 2)
        load_w(1, 2, 2)
        w2_raw = keep.tile([P, HID], BF16, name="w2_raw")
        nc.sync.dma_start(out=w2_raw[:], in_=W2g)
        for m in range(4, PAIRS):
            load_x(m)
        b2bc = keep.tile([P, OUTF], BF16, name="b2bc")
        nc.sync.dma_start(out=b2bc[:], in_=b2g.partition_broadcast(P))
        b1bc = keep.tile([P, 512], BF16, name="b1bc")
        nc.sync.dma_start(out=b1bc[:], in_=b1g[0:512].partition_broadcast(P))
        b1c_raw = keep.tile([P, 2, 2], BF16, name="b1c_raw")
        nc.sync.dma_start(out=b1c_raw[:], in_=b1g[512:1024].rearrange("(u p e) -> p u e", u=2, p=P, e=2))
        b1c = keep.tile([P, 4], F32, name="b1c")

        zeros = keep.tile([P, 512], BF16, name="zeros")
        nc.vector.memset(zeros[:].bitcast(F32), 0.0)
        ident_f = keep.tile([P, P], F32, name="ident_f")
        make_identity(nc, ident_f[:])
        ident_b = keep.tile([P, P], BF16, name="ident_b")
        make_identity(nc, ident_b[:])
        warm_in = keep.tile([P, 8], F32, name="warm_in")
        warm_out = keep.tile([P, 8], F32, name="warm_out")
        nc.vector.memset(warm_in[:], 0.0)
        nc.scalar.copy(out=warm_out[:], in_=warm_in[:])
        perm_f = keep.tile([P, P], F32, name="perm_f")
        nc.scalar.copy(out=perm_f[:].rearrange("p (j i) -> p j i", j=4), in_=ident_f[:].rearrange("p (i j) -> p j i", j=4))
        perm_b = keep.tile([P, P], BF16, name="perm_b")
        nc.scalar.copy(out=perm_b[:].rearrange("p (i j) -> p i j", j=4), in_=ident_b[:].rearrange("p (j i) -> p i j", j=4))

        w1c = [keep.tile([P, 2, 512], U32, name="w1c%d" % a, align_bytes=64) for a in range(2)]
        w1s = [keep.tile([P, 2, 512], U8, name="w1s%d" % a, align_bytes=64) for a in range(2)]
        gw = [keep.tile([P, 4096], BF16, name="gw%d" % a, align_bytes=64) for a in range(2)]
        xc = {}
        xs = {}
        for g in range(PAIRS // 2):
            xc[g] = keep.tile([P, 2, 4, P], U32, name="xc%d" % g, align_bytes=64)
            xs[g] = keep.tile([P, 2, 4, P], U8, name="xs%d" % g, align_bytes=64)
        acc0 = accp.tile([P, 512], F32, name="acc0")

        def keep_busy(count):
            for i in range(count):
                nc.tensor.matmul(acc0[:], lhsT=zeros[:, 0:P], rhs=zeros[:], start=True, stop=True)

        def transpose_words(words, identity):
            bank = tpp.tile([P, 4, P], F32, name="bank", tag="tp")
            for j in range(4):
                nc.tensor.transpose(bank[:, j, :], words[:, j * P : (j + 1) * P], identity[:])
            return bank

        def copy_out(eng, dst, bank):
            src = bank[:].rearrange("p (u k) c -> p k c u", u=2, k=2)
            if eng == "v":
                nc.vector.tensor_copy(out=dst, in_=src)
            else:
                nc.scalar.copy(out=dst, in_=src)

        def permute_words(raw, rows):
            wp = permp.tile([P, rows, 4, 4, 64], BF16, name="wp%d" % rows)
            nc.vector.tensor_copy(out=wp[:], in_=raw.rearrange("p h (q b k) -> p h b q k", q=4, b=4))
            words = wp[:].rearrange("p h b q k -> p h (b q k)").bitcast(F32)
            return [words[:, h, :] for h in range(rows)]

        w_words = {}

        def permute_w(a, t):
            raw, cnt = w_raw[(a, t)]
            words = permute_words(raw[:], cnt)
            for e in range(cnt):
                w_words[(a, t + e)] = words[e]

        def turn_w(a, t, eng):
            bank = transpose_words(w_words[(a, t)], ident_f)
            dst = gw[a][:].bitcast(F32).rearrange("p (k t c u) -> p k t c u", k=2, t=4, c=P, u=2)
            copy_out(eng, dst[:, :, t, :, :], bank)

        def quant_w(a, pair):
            for kp in range(2):
                nc.vector.quantize_mx(
                    out=w1c[a][:, kp, pair * 256 : (pair + 1) * 256].bitcast(FP8X4),
                    scales=w1s[a][:, kp, pair * 256 : (pair + 1) * 256],
                    in_=gw[a][:, kp * 2048 + pair * 1024 : kp * 2048 + (pair + 1) * 1024],
                )

        def quant_w_tile(a, t):
            for kp in range(2):
                nc.vector.quantize_mx(
                    out=w1c[a][:, kp, t * P : (t + 1) * P].bitcast(FP8X4),
                    scales=w1s[a][:, kp, t * P : (t + 1) * P],
                    in_=gw[a][:, kp * 2048 + t * 512 : kp * 2048 + (t + 1) * 512],
                )

        x_words = {}
        x_g = {}

        def stage_a(m):
            if m < NATURAL:
                x_words[m] = permute_words(x_raw[m][:], 2)
            else:
                xt = stage.tile([P, 1024], F32, name="xt", align_bytes=64)
                nc.vector.transpose(out=xt[:], in_=x_raw[m][:].rearrange("p r k -> p (r k)").bitcast(F32))
                x_words[m] = xt

        def stage_b(m, engs="ss"):
            gx = stage.tile([P, 2, 2, 512], BF16, name="gx", align_bytes=64)
            x_g[m] = gx
            if m < NATURAL:
                dst = gx[:].rearrange("p k h w -> p (k h w)").bitcast(F32).rearrange("p (k h c u) -> p h k c u", k=2, h=2, u=2)
                for h in range(2):
                    copy_out(engs[h], dst[:, h, :, :, :], transpose_words(x_words[m][h], perm_f))
            else:
                src = x_words[m][:].rearrange("p (j h u k i) -> p k h j i u", j=4, h=2, u=2, k=2, i=32)
                for kp in range(2):
                    dst = gx[:, kp, :, :].rearrange("p h w -> p (h w)").bitcast(F32)
                    nc.scalar.copy(
                        out=dst.rearrange("p (h j i u) -> p h j i u", h=2, j=4, i=32, u=2), in_=src[:, kp, :, :, :, :]
                    )

        def stage_c(m):
            s = 2 * (m % 2)
            for kp in range(2):
                nc.vector.quantize_mx(
                    out=xc[m // 2][:, kp, s : s + 2, :].rearrange("p n c -> p (n c)").bitcast(FP8X4),
                    scales=xs[m // 2][:, kp, s : s + 2, :].rearrange("p n c -> p (n c)"),
                    in_=x_g[m][:, kp, :, :].rearrange("p h w -> p (h w)"),
                )

        def first_half(m):
            for h in range(2):
                n = 2 * (m % 2) + h
                for kp in range(2):
                    nc.tensor.matmul_mx(
                        out=acc0[:],
                        lhsT=xc[m // 2][:, kp, n, :].bitcast(FP8X4),
                        lhsT_scale=xs[m // 2][:, kp, n, :],
                        rhs=w1c[0][:, kp, :].bitcast(FP8X4),
                        rhs_scale=w1s[0][:, kp, :],
                        start=(m == 0 and h == 0 and kp == 0),
                        stop=(m == PAIRS - 1 and h == 1 and kp == 1),
                    )

        sums = {}

        def second_half(g, t):
            if g == 0:
                sums[t] = tpp.tile([P, 4, P], F32, name="sum", tag="tp")
            for kp in range(2):
                nc.tensor.matmul_mx(
                    out=sums[t][:].rearrange("p s b -> p (s b)"),
                    lhsT=w1c[1][:, kp, t * P : (t + 1) * P].bitcast(FP8X4),
                    lhsT_scale=w1s[1][:, kp, t * P : (t + 1) * P],
                    rhs=xc[g][:, kp, :, :].rearrange("p s b -> p (s b)").bitcast(FP8X4),
                    rhs_scale=xs[g][:, kp, :, :].rearrange("p s b -> p (s b)"),
                    start=(g == 0 and kp == 0),
                    stop=(g == 3 and kp == 1),
                )

        def second_half_narrow(g, t):
            if g == 0:
                sums[t] = tpp.tile([P, 4, P], F32, name="sum", tag="tp")
            for n in range(4):
                for kp in range(2):
                    nc.tensor.matmul_mx(
                        out=sums[t][:, 0, :],
                        lhsT=w1c[1][:, kp, t * P : (t + 1) * P].bitcast(FP8X4),
                        lhsT_scale=w1s[1][:, kp, t * P : (t + 1) * P],
                        rhs=xc[g][:, kp, n, :].bitcast(FP8X4),
                        rhs_scale=xs[g][:, kp, n, :],
                        start=(g == 0 and n == 0 and kp == 0),
                        stop=(g == 3 and n == 3 and kp == 1),
                    )

        keep_busy(WARM)

        g2 = [keep.tile([P, P, 4], BF16, name="g2%d" % a, align_bytes=64) for a in range(2)]
        m1c = [keep.tile([P, P], U32, name="m1c%d" % a, align_bytes=64) for a in range(2)]
        m1s = [keep.tile([P, P], U8, name="m1s%d" % a, align_bytes=64) for a in range(2)]
        hid0 = keep.tile([P, 4, P], BF16, name="hid0")
        b1v = b1bc[:].rearrange("b (u p e) -> b u e p", u=2, p=P, e=2)

        def mean_bias():
            for u in range(2):
                nc.vector.scalar_tensor_tensor(
                    out=hid0[:, 2 * u : 2 * u + 2, :],
                    in0=acc0[:].rearrange("b (t p) -> b t p", t=4)[:, 2 * u : 2 * u + 2, :],
                    scalar=1.0 / NODES,
                    in1=b1v[:, u, :, :],
                    op0=ALU.mult,
                    op1=ALU.add,
                )

        def turn_hidden():
            hid_t = tpp.tile([P, 4, P], BF16, name="hidT", tag="tp")
            for t in range(4):
                nc.tensor.transpose(hid_t[:, t, :], hid0[:, t, :], perm_b[:])
            nc.scalar.activation(out=g2[0][:], in_=hid_t[:].rearrange("p t b -> p b t"), func=ACTF.Relu)

        def quant_hidden(a):
            nc.vector.quantize_mx(
                out=m1c[a][:].bitcast(FP8X4), scales=m1s[a][:], in_=g2[a][:].rearrange("p b t -> p (b t)")
            )

        def finish(t, wide):
            if wide:
                total = stage.tile([P, P], F32, name="total")
                nc.vector.tensor_reduce(
                    out=total[:], in_=sums[t][:].rearrange("p s b -> p b s"), axis=AXIS_X, op=ALU.add
                )
                total = total[:]
            else:
                total = sums[t][:, 0, :]
            nc.scalar.activation(
                out=g2[1][:, :, t].rearrange("p (i j) -> p i j", j=4),
                in_=total.rearrange("p (j i) -> p i j", j=4),
                func=ACTF.Relu,
                bias=b1c[:, t : t + 1],
                scale=1.0 / NODES,
            )

        acc2 = accp.tile([P, OUTF], F32, name="acc2")

        def layer2(a):
            nc.tensor.matmul_mx(
                out=acc2[:],
                lhsT=m1c[a][:].bitcast(FP8X4),
                lhsT_scale=m1s[a][:],
                rhs=w2c[:, a, :].bitcast(FP8X4),
                rhs_scale=w2s[:, a, :],
                start=(a == 0),
                stop=(a == 1),
            )

        w2_state = {}

        def turn_w2():
            w2bank = transpose_words(w2_raw[:].bitcast(F32), ident_f)
            gw2 = keep.tile([P, 1024], BF16, name="gw2", align_bytes=64)
            nc.scalar.copy(
                out=gw2[:].bitcast(F32).rearrange("p (k c u) -> p k c u", k=2, c=P, u=2),
                in_=w2bank[:].rearrange("p (k u) c -> p k c u", k=2, u=2),
            )
            w2_state["g"] = gw2

        def quant_w2():
            nc.vector.quantize_mx(
                out=w2c[:].rearrange("p k c -> p (k c)").bitcast(FP8X4),
                scales=w2s[:].rearrange("p k c -> p (k c)"),
                in_=w2_state["g"][:],
            )

        w2c = keep.tile([P, 2, P], U32, name="w2c", align_bytes=64)
        w2s = keep.tile([P, 2, P], U8, name="w2s", align_bytes=64)

        permute_w(0, 0)
        stage_a(0)
        permute_w(0, 1)
        turn_w(0, 0, "s")
        permute_w(0, 2)
        quant_w_tile(0, 0)
        permute_w(0, 3)
        stage_b(0, "sv")
        turn_w(0, 1, "s")
        stage_a(1)
        stage_c(0)
        turn_w(0, 2, "s")
        stage_a(2)
        turn_w(0, 3, "s")
        quant_w_tile(0, 1)
        stage_b(1)
        stage_a(3)
        stage_b(2)
        quant_w_tile(0, 2)
        quant_w_tile(0, 3)
        stage_c(1)
        stage_b(3)
        first_half(0)
        permute_w(1, 0)
        permute_w(1, 2)
        first_half(1)
        for t in range(4):
            turn_w(1, t, "s")
        turn_w2()
        stage_c(2)
        stage_c(3)
        first_half(2)
        quant_w(1, 0)
        stage_a(4)
        stage_b(4)
        quant_w(1, 1)
        stage_a(5)
        first_half(3)
        stage_b(5)
        stage_c(4)
        quant_w2()
        def second(g):
            for t in range(3):
                second_half(g, t)
            if g < 2:
                second_half_narrow(g, 3)
        for g in range(2):
            second(g)
        stage_a(6)
        stage_b(6)
        first_half(4)
        stage_c(5)
        first_half(5)
        stage_a(7)
        stage_b(7)
        stage_c(6)
        second(2)
        first_half(6)
        stage_c(7)
        first_half(7)
        nc.vector.tensor_copy(out=b1c[:], in_=b1c_raw[:].rearrange("p u e -> p (u e)"))
        mean_bias()
        second_half(3, 0)
        finish(0, True)
        second_half(3, 1)
        turn_hidden()
        finish(1, True)
        second_half(3, 2)
        finish(2, True)
        for g in range(2, 4):
            second_half_narrow(g, 3)
        quant_hidden(0)
        layer2(0)
        finish(3, False)
        quant_hidden(1)
        layer2(1)

        pre = keep.tile([P, OUTF], F32, name="pre")
        nc.vector.tensor_tensor(out=pre[:], in0=acc2[:], in1=b2bc[:], op=ALU.add)
        m2r = keep.tile([P, REP, OUTF], F32, name="m2r")
        nc.vector.tensor_scalar_max(
            out=m2r[:], in0=pre[:].unsqueeze(1).to_broadcast([P, REP, OUTF]), scalar1=0.0
        )
        nc.sync.dma_start(
            out=out.rearrange("b (i r) o -> b i (r o)", r=REP),
            in_=m2r[:].rearrange("p r o -> p (r o)").unsqueeze(1).to_broadcast([P, NODES // REP, REP * OUTF]),
        )
